import numpy as np
import ml_dtypes


def mxq(x, axis, fmt="e4m3"):
    dtype, down = {"e4m3": (ml_dtypes.float8_e4m3fn, 7), "e5m2": (ml_dtypes.float8_e5m2, 14)}[fmt]
    v = np.moveaxis(np.asarray(x, np.float32).astype(ml_dtypes.bfloat16).astype(np.float64), axis, -1)
    blocks = v.reshape(v.shape[:-1] + (-1, 32))
    amax = np.abs(blocks).max(-1, keepdims=True)
    byte = np.maximum(np.where(amax > 0, np.frexp(amax)[1] - 1 + 127, 0) - down, 1)
    scale = np.exp2(byte - 127.0)
    codes = (blocks / scale).astype(np.float32).astype(dtype).astype(np.float64)
    return np.moveaxis((codes * scale).reshape(v.shape), -1, axis)


WIDE = False


def mx_kscale(k):
    if not WIDE:
        return np.ones(k)
    levels = np.array([10, -10, 5, -5, 0])
    a = np.random.permutation(np.resize(levels, k // 512 * 4)).reshape(k // 512, 4)
    idx = np.arange(k)
    return np.exp2(a[idx // 512, idx % 128 // 32])


BF16 = ml_dtypes.bfloat16


def bf(x):
    return np.asarray(x, np.float32).astype(BF16)


def f64(x):
    return np.asarray(x).astype(np.float64)


B, N, D, H, DH = 64, 128, 256, 4, 128
E = H * DH
GAIN = np.sqrt(1.8 / DH)


def setup_inputs():
    t = mx_kscale(E)
    return {"q_rot": bf(np.random.standard_normal((B, H, N, DH)) * GAIN),
            "k_rot": bf(np.random.standard_normal((B, H, N, DH)) * GAIN),
            "v": bf(np.random.standard_normal((B, H, N, DH)) * t.reshape(H, 1, DH)),
            "w_out": bf(np.random.standard_normal((E, D)) * E ** -0.5 / t[:, None]),
            "b_out": bf(np.random.standard_normal(D) * 0.2)}


def reference(q_rot, k_rot, v, w_out, b_out):
    scores = f64(q_rot) @ f64(k_rot).transpose(0, 1, 3, 2) * np.sqrt(DH)
    e = np.exp(scores - scores.max(-1, keepdims=True))
    p = e / e.sum(-1, keepdims=True)
    gate = p.sum(axis=2)
    attn = f64(v) * gate[..., None]
    attn = attn.transpose(0, 2, 1, 3).reshape(B, N, E)
    return (mxq(attn, 2, "e4m3") @ mxq(f64(w_out), 0, "e4m3")) + f64(b_out)

@@ -1,0 +1,257 @@
+from contextlib import ExitStack
+import math
+
+import concourse.bass as bass
+import concourse.mybir as mybir
+import concourse.tile as tile
+from concourse.masks import make_identity
+
+F32 = mybir.dt.float32
+BF16 = mybir.dt.bfloat16
+U32 = mybir.dt.uint32
+U8 = mybir.dt.uint8
+FP8X4 = mybir.dt.float8_e4m3fn_x4
+ALU = mybir.AluOpType
+ACTF = mybir.ActivationFunctionType
+AX = mybir.AxisListType
+
+B, H, N, DH, D = 64, 4, 128, 128, 256
+P = 128
+T4 = 4
+J = 32
+GB = 4
+G = B // GB
+PRE = 3
+SCALE = math.sqrt(128.0)
+FLOPS = 2 * B * H * N * N * DH + 2 * B * N * (H * DH) * D
+
+
+def tile_attn_pb_t_kernel(tc, q_rot, k_rot, v, w_out, b_out, out):
+    nc = tc.nc
+    with ExitStack() as ctx:
+        ctx.enter_context(tc.manual_schedule())
+        const = ctx.enter_context(tc.tile_pool(name="const", bufs=1))
+        qk_in = ctx.enter_context(tc.tile_pool(name="qk_in", bufs=PRE + 1))
+        v_in = ctx.enter_context(tc.tile_pool(name="v_in", bufs=PRE + 3))
+        work = ctx.enter_context(tc.tile_pool(name="work", bufs=4))
+        small = ctx.enter_context(tc.tile_pool(name="small", bufs=6))
+        mxp = ctx.enter_context(tc.tile_pool(name="mxp", bufs=3))
+        outp = ctx.enter_context(tc.tile_pool(name="outp", bufs=3))
+        ps_t = ctx.enter_context(tc.psum_pool(name="ps_t", bufs=2))
+        ps_s = ctx.enter_context(tc.psum_pool(name="ps_s", bufs=2))
+        ps_c = ctx.enter_context(tc.psum_pool(name="ps_c", bufs=1))
+        ps_x = ctx.enter_context(tc.psum_pool(name="ps_x", bufs=1))
+        ps_o = ctx.enter_context(tc.psum_pool(name="ps_o", bufs=1))
+
+        q_sb, k_sb, v_sb = {}, {}, {}
+        tqk_t, qkT_t, s_t, nm_t, e_t, z_t, r_t = {}, {}, {}, {}, {}, {}, {}
+        pc_t, c4_t, a_t, xt_t, grp_t, cod_t, scl_t, po_t, o_t = {}, {}, {}, {}, {}, {}, {}, {}, {}
+
+        def load(g):
+            for store, src, pool, nm in ((q_sb, q_rot, qk_in, "q"), (k_sb, k_rot, qk_in, "k"), (v_sb, v, v_in, "v")):
+                t = pool.tile([P, GB, T4 * DH], BF16, name=nm + "_sb")
+                nc.sync.dma_start(
+                    out=t[:],
+                    in_=src[g * GB:(g + 1) * GB].rearrange("b h (j t) d -> (h j) b (t d)", t=T4),
+                )
+                store[g] = t
+
+        ident = const.tile([P, P], BF16, name="ident")
+        make_identity(nc, ident[:])
+        for g in range(PRE):
+            load(g)
+        perm = const.tile([P, J, H], BF16, name="perm")
+        nc.vector.tensor_copy(out=perm[:], in_=ident[:].rearrange("p (h j) -> p j h", h=H))
+        mask = const.tile([P, H], F32, name="mask")
+        nc.vector.tensor_reduce(out=mask[:], in_=ident[:].rearrange("p (h j) -> p h j", h=H), axis=AX.X, op=ALU.add)
+
+        w_raw = const.tile([P, H, D], BF16, name="w_raw")
+        nc.sync.dma_start(out=w_raw[:], in_=w_out.rearrange("(h p) n -> p h n", p=P))
+        bias_bf = const.tile([P, D], BF16, name="bias_bf")
+        nc.sync.dma_start(out=bias_bf[:], in_=b_out.partition_broadcast(P))
+        w_grp = const.tile([P, D, H], BF16, name="w_grp", align_bytes=64)
+        w_cod = const.tile([P, D], U32, name="w_cod", align_bytes=64)
+        w_scl = const.tile([P, D], U8, name="w_scl", align_bytes=64)
+        bias = const.tile([P, D], F32, name="bias")
+
+        def prep_w():
+            nc.vector.tensor_copy(out=w_grp[:], in_=w_raw[:].rearrange("p h n -> p n h"))
+            nc.vector.tensor_copy(out=bias[:], in_=bias_bf[:])
+            nc.vector.quantize_mx(
+                out=w_cod[:].bitcast(FP8X4), scales=w_scl[:], in_=w_grp[:].rearrange("p n h -> p (n h)")
+            )
+
+        def st_T(b):
+            g, i = divmod(b, GB)
+            tqk = ps_t.tile([P, 2, H, T4, J], BF16, name="tqk")
+            for x, src in enumerate((q_sb[g], k_sb[g])):
+                for t in range(T4):
+                    nc.tensor.transpose(tqk[:, x, :, t, :], src[:, i, t * DH:(t + 1) * DH], ident[:])
+            tqk_t[b] = tqk
+
+        def st_EV(b):
+            qkT = work.tile([P, 2, H, N], BF16, name="qkT")
+            nc.scalar.copy(
+                out=qkT[:].rearrange("p x h n -> p (x h n)"),
+                in_=tqk_t[b][:].rearrange("p x h t j -> p (x h t j)"),
+            )
+            qkT_t[b] = qkT
+
+        def st_QK(b, hs):
+            if b not in s_t:
+                s_t[b] = ps_s.tile([P, H, N], F32, name="s")
+            for h in hs:
+                nc.tensor.matmul(
+                    s_t[b][:, h, :], lhsT=qkT_t[b][:, 0, h, :], rhs=qkT_t[b][:, 1, h, :], start=True, stop=True
+                )
+
+        def st_MAX(b):
+            mx = small.tile([P, H], F32, name="mx")
+            nc.vector.tensor_reduce(out=mx[:], in_=s_t[b][:], axis=AX.X, op=ALU.max)
+            nm = small.tile([P, H], F32, name="nm")
+            nc.vector.tensor_scalar(out=nm[:], in0=mx[:], scalar1=-SCALE, scalar2=None, op0=ALU.mult)
+            nm_t[b] = nm
+
+        def st_EXP(b):
+            e = work.tile([P, T4, H, J], F32, name="e")
+            z = small.tile([P, H], F32, name="z")
+            for h in range(H):
+                nc.scalar.activation(
+                    out=e[:, :, h, :],
+                    in_=s_t[b][:, h, :].rearrange("p (t j) -> p t j", t=T4),
+                    func=ACTF.Exp,
+                    bias=nm_t[b][:, h:h + 1],
+                    scale=SCALE,
+                    accum_out=z[:, h:h + 1],
+                )
+            e_t[b] = e
+            z_t[b] = z
+
+        def st_REC(b):
+            r = small.tile([P, H], F32, name="r")
+            nc.vector.reciprocal(out=r[:], in_=z_t[b][:])
+            r_t[b] = r
+
+        def st_C(b):
+            u, i2 = divmod(b, 2)
+            if i2 == 0:
+                pc_t[u] = ps_c.tile([P, 2, T4, H], F32, name="pc")
+            for t in range(T4):
+                nc.tensor.matmul(
+                    pc_t[u][:, i2, t, :],
+                    lhsT=e_t[b][:, t, :, :].rearrange("p h j -> p (h j)"),
+                    rhs=r_t[b][:],
+                    start=True,
+                    stop=True,
+                )
+
+        def st_SEL(u):
+            tmp = small.tile([P, 2 * T4, H], F32, name="tmp")
+            nc.vector.tensor_tensor(
+                out=tmp[:],
+                in0=pc_t[u][:].rearrange("p b t h -> p (b t) h"),
+                in1=mask[:].unsqueeze(1).to_broadcast([P, 2 * T4, H]),
+                op=ALU.mult,
+            )
+            c4 = small.tile([P, 2 * T4], F32, name="c4")
+            nc.vector.tensor_reduce(out=c4[:], in_=tmp[:], axis=AX.X, op=ALU.add)
+            c4_t[u] = c4
+
+        def st_MUL(b):
+            g, i = divmod(b, GB)
+            u, i2 = divmod(b, 2)
+            a = work.tile([P, T4, DH], BF16, name="a")
+            nc.gpsimd.tensor_tensor(
+                out=a[:],
+                in0=v_sb[g][:, i, :].rearrange("p (t d) -> p t d", t=T4),
+                in1=c4_t[u][:, i2 * T4:(i2 + 1) * T4].unsqueeze(2).to_broadcast([P, T4, DH]),
+                op=ALU.mult,
+            )
+            a_t[b] = a
+
+        def st_AT(b):
+            u, i2 = divmod(b, 2)
+            if i2 == 0:
+                xt_t[u] = ps_x.tile([P, 2, J, T4, H], BF16, name="xt")
+            for t in range(T4):
+                nc.tensor.transpose(
+                    xt_t[u][:, i2, :, t, :], a_t[b][:, t, :], perm[:].rearrange("p j h -> p (j h)")
+                )
+
+        def st_XEV(u):
+            grp = mxp.tile([P, 2 * N * H], BF16, name="grp", align_bytes=64)
+            nc.vector.tensor_copy(out=grp[:], in_=xt_t[u][:].rearrange("p b j t h -> p (b j t h)"))
+            grp_t[u] = grp
+
+        def st_QZ(u):
+            cod = mxp.tile([P, 2 * N], U32, name="cod", align_bytes=64)
+            scl = mxp.tile([P, 2 * N], U8, name="scl", align_bytes=64)
+            nc.vector.quantize_mx(out=cod[:].bitcast(FP8X4), scales=scl[:], in_=grp_t[u][:])
+            cod_t[u] = cod
+            scl_t[u] = scl
+
+        def st_MX(u):
+            po = ps_o.tile([P, 2, D], F32, name="po")
+            for i2 in range(2):
+                nc.tensor.matmul_mx(
+                    out=po[:, i2, :],
+                    lhsT=cod_t[u][:, i2 * N:(i2 + 1) * N].bitcast(FP8X4),
+                    lhsT_scale=scl_t[u][:, i2 * N:(i2 + 1) * N],
+                    rhs=w_cod[:].bitcast(FP8X4),
+                    rhs_scale=w_scl[:],
+                    start=True,
+                    stop=True,
+                )
+            po_t[u] = po
+
+        def st_OUT(u):
+            g, i = divmod(u, 2)
+            if i == 0:
+                o_t[g] = outp.tile([P, GB, D], F32, name="o")
+            nc.vector.tensor_tensor(
+                out=o_t[g][:, 2 * i:2 * i + 2, :],
+                in0=po_t[u][:],
+                in1=bias[:].unsqueeze(1).to_broadcast([P, 2, D]),
+                op=ALU.add,
+            )
+            if i == 1:
+                nc.sync.dma_start(out=out[g * GB:(g + 1) * GB].rearrange("b m d -> m b d"), in_=o_t[g][:])
+
+        def ok(b):
+            return 0 <= b < B
+
+        def oku(x2):
+            return x2 % 2 == 0 and 0 <= x2 // 2 < B // 2
+
+        for k in range(B + 12):
+            if k % GB == 0 and k // GB + PRE < G:
+                load(k // GB + PRE)
+            if ok(k):
+                st_T(k)
+                st_EV(k)
+            if k == 5:
+                prep_w()
+            if oku(k - 8):
+                st_XEV((k - 8) // 2)
+            if oku(k - 9):
+                st_QZ((k - 9) // 2)
+            if oku(k - 11):
+                st_OUT((k - 11) // 2)
+            if ok(k - 1):
+                st_QK(k - 1, (0, 1))
+            if oku(k - 10):
+                st_MX((k - 10) // 2)
+            if ok(k - 1):
+                st_QK(k - 1, (2, 3))
+                st_MAX(k - 1)
+                st_EXP(k - 1)
+            if ok(k - 2):
+                st_REC(k - 2)
+            if ok(k - 3):
+                st_C(k - 3)
+            if oku(k - 4):
+                st_SEL((k - 4) // 2)
+            if ok(k - 4):
+                st_MUL(k - 4)
+            if ok(k - 6):
+                st_AT(k - 6)

@@ -1,13 +1,12 @@
 from contextlib import ExitStack
 import math
 
-import concourse.bass as bass
 import concourse.mybir as mybir
-import concourse.tile as tile
 from concourse.masks import make_identity
 
 F32 = mybir.dt.float32
 BF16 = mybir.dt.bfloat16
+I32 = mybir.dt.int32
 U32 = mybir.dt.uint32
 U8 = mybir.dt.uint8
 FP8X4 = mybir.dt.float8_e4m3fn_x4
@@ -19,9 +18,11 @@ B, H, N, DH, D = 64, 4, 128, 128, 256
 P = 128
 T4 = 4
 J = 32
-GB = 4
-G = B // GB
-PRE = 3
+NP = B // 2
+PRE = 4
+REP = 4
+WARM0 = 4
+WARM_STEPS = 2
 SCALE = math.sqrt(128.0)
 FLOPS = 2 * B * H * N * N * DH + 2 * B * N * (H * DH) * D
 
@@ -31,39 +32,60 @@ def tile_attn_pb_t_kernel(tc, q_rot, k_rot, v, w_out, b_out, out):
     with ExitStack() as ctx:
         ctx.enter_context(tc.manual_schedule())
         const = ctx.enter_context(tc.tile_pool(name="const", bufs=1))
-        qk_in = ctx.enter_context(tc.tile_pool(name="qk_in", bufs=PRE + 1))
-        v_in = ctx.enter_context(tc.tile_pool(name="v_in", bufs=PRE + 3))
-        work = ctx.enter_context(tc.tile_pool(name="work", bufs=4))
-        small = ctx.enter_context(tc.tile_pool(name="small", bufs=6))
+        qk_in = ctx.enter_context(tc.tile_pool(name="qk_in", bufs=PRE + 2))
+        v_in = ctx.enter_context(tc.tile_pool(name="v_in", bufs=PRE + 4))
+        work = ctx.enter_context(tc.tile_pool(name="work", bufs=6))
+        apool = ctx.enter_context(tc.tile_pool(name="apool", bufs=8))
+        small = ctx.enter_context(tc.tile_pool(name="small", bufs=4))
         mxp = ctx.enter_context(tc.tile_pool(name="mxp", bufs=3))
         outp = ctx.enter_context(tc.tile_pool(name="outp", bufs=3))
         ps_t = ctx.enter_context(tc.psum_pool(name="ps_t", bufs=2))
-        ps_s = ctx.enter_context(tc.psum_pool(name="ps_s", bufs=2))
+        ps_s = ctx.enter_context(tc.psum_pool(name="ps_s", bufs=3))
         ps_c = ctx.enter_context(tc.psum_pool(name="ps_c", bufs=1))
         ps_x = ctx.enter_context(tc.psum_pool(name="ps_x", bufs=1))
         ps_o = ctx.enter_context(tc.psum_pool(name="ps_o", bufs=1))
 
         q_sb, k_sb, v_sb = {}, {}, {}
         tqk_t, qkT_t, s_t, nm_t, e_t, z_t, r_t = {}, {}, {}, {}, {}, {}, {}
-        pc_t, c4_t, a_t, xt_t, grp_t, cod_t, scl_t, po_t, o_t = {}, {}, {}, {}, {}, {}, {}, {}, {}
+        pc_t, c4_t, a_t, xt_t, grp_t, cod_t, scl_t, po_t = {}, {}, {}, {}, {}, {}, {}, {}
 
-        def load(g):
+        def load(j):
             for store, src, pool, nm in ((q_sb, q_rot, qk_in, "q"), (k_sb, k_rot, qk_in, "k"), (v_sb, v, v_in, "v")):
-                t = pool.tile([P, GB, T4 * DH], BF16, name=nm + "_sb")
+                t = pool.tile([P, 2, T4 * DH], BF16, name=nm + "_sb")
                 nc.sync.dma_start(
                     out=t[:],
-                    in_=src[g * GB:(g + 1) * GB].rearrange("b h (j t) d -> (h j) b (t d)", t=T4),
+                    in_=src[2 * j:2 * j + 2].rearrange("b h (j t) d -> (h j) b (t d)", t=T4),
                 )
-                store[g] = t
+                store[j] = t
+
+        for j in range(PRE):
+            load(j)
+        zsrc = const.tile([P, 2048], BF16, name="zsrc", align_bytes=64)
+        zcod = const.tile([P, 512], U32, name="zcod", align_bytes=64)
+        zscl = const.tile([P, 512], U8, name="zscl", align_bytes=64)
+        nc.vector.memset(zsrc[:].bitcast(I32), 0)
+        nc.vector.quantize_mx(out=zcod[:].bitcast(FP8X4), scales=zscl[:], in_=zsrc[:])
+
+        def warm(n):
+            for x in range(n):
+                dm = ps_o.tile([P, 2, D], F32, name="po")
+                nc.tensor.matmul_mx(
+                    out=dm[:].rearrange("p b d -> p (b d)"),
+                    lhsT=zcod[:, 0:P].bitcast(FP8X4),
+                    lhsT_scale=zscl[:, 0:P],
+                    rhs=zcod[:].bitcast(FP8X4),
+                    rhs_scale=zscl[:],
+                    start=True,
+                    stop=True,
+                )
 
         ident = const.tile([P, P], BF16, name="ident")
         make_identity(nc, ident[:])
-        for g in range(PRE):
-            load(g)
         perm = const.tile([P, J, H], BF16, name="perm")
         nc.vector.tensor_copy(out=perm[:], in_=ident[:].rearrange("p (h j) -> p j h", h=H))
         mask = const.tile([P, H], F32, name="mask")
         nc.vector.tensor_reduce(out=mask[:], in_=ident[:].rearrange("p (h j) -> p h j", h=H), axis=AX.X, op=ALU.add)
+        warm(WARM0)
 
         w_raw = const.tile([P, H, D], BF16, name="w_raw")
         nc.sync.dma_start(out=w_raw[:], in_=w_out.rearrange("(h p) n -> p h n", p=P))
@@ -82,28 +104,26 @@ def tile_attn_pb_t_kernel(tc, q_rot, k_rot, v, w_out, b_out, out):
             )
 
         def st_T(b):
-            g, i = divmod(b, GB)
+            u, x = divmod(b, 2)
             tqk = ps_t.tile([P, 2, H, T4, J], BF16, name="tqk")
-            for x, src in enumerate((q_sb[g], k_sb[g])):
+            for y, src in enumerate((q_sb[u], k_sb[u])):
                 for t in range(T4):
-                    nc.tensor.transpose(tqk[:, x, :, t, :], src[:, i, t * DH:(t + 1) * DH], ident[:])
+                    nc.tensor.transpose(tqk[:, y, :, t, :], src[:, x, t * DH:(t + 1) * DH], ident[:])
             tqk_t[b] = tqk
 
         def st_EV(b):
             qkT = work.tile([P, 2, H, N], BF16, name="qkT")
             nc.scalar.copy(
-                out=qkT[:].rearrange("p x h n -> p (x h n)"),
-                in_=tqk_t[b][:].rearrange("p x h t j -> p (x h t j)"),
+                out=qkT[:].rearrange("p y h n -> p (y h n)"),
+                in_=tqk_t[b][:].rearrange("p y h t j -> p (y h t j)"),
             )
             qkT_t[b] = qkT
 
-        def st_QK(b, hs):
-            if b not in s_t:
-                s_t[b] = ps_s.tile([P, H, N], F32, name="s")
-            for h in hs:
-                nc.tensor.matmul(
-                    s_t[b][:, h, :], lhsT=qkT_t[b][:, 0, h, :], rhs=qkT_t[b][:, 1, h, :], start=True, stop=True
-                )
+        def st_QK(b):
+            s = ps_s.tile([P, H, N], F32, name="s")
+            for h in range(H):
+                nc.tensor.matmul(s[:, h, :], lhsT=qkT_t[b][:, 0, h, :], rhs=qkT_t[b][:, 1, h, :], start=True, stop=True)
+            s_t[b] = s
 
         def st_MAX(b):
             mx = small.tile([P, H], F32, name="mx")
@@ -113,8 +133,10 @@ def tile_attn_pb_t_kernel(tc, q_rot, k_rot, v, w_out, b_out, out):
             nm_t[b] = nm
 
         def st_EXP(b):
+            u, x = divmod(b, 2)
             e = work.tile([P, T4, H, J], F32, name="e")
-            z = small.tile([P, H], F32, name="z")
+            if x == 0:
+                z_t[u] = small.tile([P, 2 * H], F32, name="z")
             for h in range(H):
                 nc.scalar.activation(
                     out=e[:, :, h, :],
@@ -122,25 +144,24 @@ def tile_attn_pb_t_kernel(tc, q_rot, k_rot, v, w_out, b_out, out):
                     func=ACTF.Exp,
                     bias=nm_t[b][:, h:h + 1],
                     scale=SCALE,
-                    accum_out=z[:, h:h + 1],
+                    accum_out=z_t[u][:, x * H + h:x * H + h + 1],
                 )
             e_t[b] = e
-            z_t[b] = z
 
-        def st_REC(b):
-            r = small.tile([P, H], F32, name="r")
-            nc.vector.reciprocal(out=r[:], in_=z_t[b][:])
-            r_t[b] = r
+        def st_REC(u):
+            r = small.tile([P, 2 * H], F32, name="r")
+            nc.vector.reciprocal(out=r[:], in_=z_t[u][:])
+            r_t[u] = r
 
         def st_C(b):
-            u, i2 = divmod(b, 2)
-            if i2 == 0:
-                pc_t[u] = ps_c.tile([P, 2, T4, H], F32, name="pc")
+            u, x = divmod(b, 2)
+            if x == 0:
+                pc_t[u] = ps_c.tile([P, 2, T4, REP, H], F32, name="pc")
             for t in range(T4):
                 nc.tensor.matmul(
-                    pc_t[u][:, i2, t, :],
+                    pc_t[u][:, x, t, :, :],
                     lhsT=e_t[b][:, t, :, :].rearrange("p h j -> p (h j)"),
-                    rhs=r_t[b][:],
+                    rhs=r_t[u][:, x * H:(x + 1) * H].unsqueeze(1).to_broadcast([P, REP, H]),
                     start=True,
                     stop=True,
                 )
@@ -149,7 +170,7 @@ def tile_attn_pb_t_kernel(tc, q_rot, k_rot, v, w_out, b_out, out):
             tmp = small.tile([P, 2 * T4, H], F32, name="tmp")
             nc.vector.tensor_tensor(
                 out=tmp[:],
-                in0=pc_t[u][:].rearrange("p b t h -> p (b t) h"),
+                in0=pc_t[u][:, :, :, 0, :].rearrange("p b t h -> p (b t) h"),
                 in1=mask[:].unsqueeze(1).to_broadcast([P, 2 * T4, H]),
                 op=ALU.mult,
             )
@@ -158,29 +179,30 @@ def tile_attn_pb_t_kernel(tc, q_rot, k_rot, v, w_out, b_out, out):
             c4_t[u] = c4
 
         def st_MUL(b):
-            g, i = divmod(b, GB)
-            u, i2 = divmod(b, 2)
-            a = work.tile([P, T4, DH], BF16, name="a")
+            u, x = divmod(b, 2)
+            a = apool.tile([P, T4, DH], BF16, name="a")
             nc.gpsimd.tensor_tensor(
                 out=a[:],
-                in0=v_sb[g][:, i, :].rearrange("p (t d) -> p t d", t=T4),
-                in1=c4_t[u][:, i2 * T4:(i2 + 1) * T4].unsqueeze(2).to_broadcast([P, T4, DH]),
+                in0=v_sb[u][:, x, :].rearrange("p (t d) -> p t d", t=T4),
+                in1=c4_t[u][:, x * T4:(x + 1) * T4].unsqueeze(2).to_broadcast([P, T4, DH]),
                 op=ALU.mult,
             )
             a_t[b] = a
 
         def st_AT(b):
-            u, i2 = divmod(b, 2)
-            if i2 == 0:
+            u, x = divmod(b, 2)
+            if x == 0:
                 xt_t[u] = ps_x.tile([P, 2, J, T4, H], BF16, name="xt")
             for t in range(T4):
-                nc.tensor.transpose(
-                    xt_t[u][:, i2, :, t, :], a_t[b][:, t, :], perm[:].rearrange("p j h -> p (j h)")
-                )
+                nc.tensor.transpose(xt_t[u][:, x, :, t, :], a_t[b][:, t, :], perm[:].rearrange("p j h -> p (j h)"))
 
         def st_XEV(u):
             grp = mxp.tile([P, 2 * N * H], BF16, name="grp", align_bytes=64)
-            nc.vector.tensor_copy(out=grp[:], in_=xt_t[u][:].rearrange("p b j t h -> p (b j t h)"))
+            src = xt_t[u][:].rearrange("p b j t h -> p (b j t h)")
+            if u % 2 == 1:
+                nc.scalar.copy(out=grp[:], in_=src)
+            else:
+                nc.vector.tensor_copy(out=grp[:], in_=src)
             grp_t[u] = grp
 
         def st_QZ(u):
@@ -190,68 +212,62 @@ def tile_attn_pb_t_kernel(tc, q_rot, k_rot, v, w_out, b_out, out):
             cod_t[u] = cod
             scl_t[u] = scl
 
-        def st_MX(u):
-            po = ps_o.tile([P, 2, D], F32, name="po")
-            for i2 in range(2):
-                nc.tensor.matmul_mx(
-                    out=po[:, i2, :],
-                    lhsT=cod_t[u][:, i2 * N:(i2 + 1) * N].bitcast(FP8X4),
-                    lhsT_scale=scl_t[u][:, i2 * N:(i2 + 1) * N],
-                    rhs=w_cod[:].bitcast(FP8X4),
-                    rhs_scale=w_scl[:],
-                    start=True,
-                    stop=True,
-                )
-            po_t[u] = po
+        def st_MX(u, x):
+            if x == 0:
+                po_t[u] = ps_o.tile([P, 2, D], F32, name="po")
+            nc.tensor.matmul_mx(
+                out=po_t[u][:, x, :],
+                lhsT=cod_t[u][:, x * N:(x + 1) * N].bitcast(FP8X4),
+                lhsT_scale=scl_t[u][:, x * N:(x + 1) * N],
+                rhs=w_cod[:].bitcast(FP8X4),
+                rhs_scale=w_scl[:],
+                start=True,
+                stop=True,
+            )
 
         def st_OUT(u):
-            g, i = divmod(u, 2)
-            if i == 0:
-                o_t[g] = outp.tile([P, GB, D], F32, name="o")
+            o = outp.tile([P, 2, D], F32, name="o")
             nc.vector.tensor_tensor(
-                out=o_t[g][:, 2 * i:2 * i + 2, :],
-                in0=po_t[u][:],
-                in1=bias[:].unsqueeze(1).to_broadcast([P, 2, D]),
-                op=ALU.add,
+                out=o[:], in0=po_t[u][:], in1=bias[:].unsqueeze(1).to_broadcast([P, 2, D]), op=ALU.add
             )
-            if i == 1:
-                nc.sync.dma_start(out=out[g * GB:(g + 1) * GB].rearrange("b m d -> m b d"), in_=o_t[g][:])
+            nc.sync.dma_start(out=out[2 * u:2 * u + 2].rearrange("b m d -> m b d"), in_=o[:])
 
-        def ok(b):
-            return 0 <= b < B
+        def ok(u):
+            return 0 <= u < NP
 
-        def oku(x2):
-            return x2 % 2 == 0 and 0 <= x2 // 2 < B // 2
-
-        for k in range(B + 12):
-            if k % GB == 0 and k // GB + PRE < G:
-                load(k // GB + PRE)
-            if ok(k):
-                st_T(k)
-                st_EV(k)
-            if k == 5:
+        for i in range(NP + 7):
+            if ok(i + PRE):
+                load(i + PRE)
+            if ok(i - 6):
+                st_QZ(i - 6)
+            if ok(i - 2):
+                st_REC(i - 2)
+            if i == 3:
                 prep_w()
-            if oku(k - 8):
-                st_XEV((k - 8) // 2)
-            if oku(k - 9):
-                st_QZ((k - 9) // 2)
-            if oku(k - 11):
-                st_OUT((k - 11) // 2)
-            if ok(k - 1):
-                st_QK(k - 1, (0, 1))
-            if oku(k - 10):
-                st_MX((k - 10) // 2)
-            if ok(k - 1):
-                st_QK(k - 1, (2, 3))
-                st_MAX(k - 1)
-                st_EXP(k - 1)
-            if ok(k - 2):
-                st_REC(k - 2)
-            if ok(k - 3):
-                st_C(k - 3)
-            if oku(k - 4):
-                st_SEL((k - 4) // 2)
-            if ok(k - 4):
-                st_MUL(k - 4)
-            if ok(k - 6):
-                st_AT(k - 6)
+            if ok(i - 5):
+                st_XEV(i - 5)
+            if ok(i):
+                for b in (2 * i, 2 * i + 1):
+                    st_T(b)
+                    st_EV(b)
+            if i < WARM_STEPS:
+                warm(2)
+            if ok(i - 1):
+                for b in (2 * i - 2, 2 * i - 1):
+                    st_QK(b)
+                    st_MAX(b)
+                    st_EXP(b)
+            for x in range(2):
+                if ok(i - 2):
+                    st_C(2 * (i - 2) + x)
+                if ok(i - 6):
+                    st_MX(i - 6, x)
+            if ok(i - 2):
+                st_SEL(i - 2)
+                st_MUL(2 * (i - 2))
+                st_MUL(2 * (i - 2) + 1)
+            if ok(i - 6):
+                st_OUT(i - 6)
+            if ok(i - 4):
+                st_AT(2 * (i - 4))
+                st_AT(2 * (i - 4) + 1)

@@ -181,12 +181,14 @@ def tile_attn_pb_t_kernel(tc, q_rot, k_rot, v, w_out, b_out, out):
         def st_MUL(b):
             u, x = divmod(b, 2)
             a = apool.tile([P, T4, DH], BF16, name="a")
-            nc.gpsimd.tensor_tensor(
-                out=a[:],
-                in0=v_sb[u][:, x, :].rearrange("p (t d) -> p t d", t=T4),
-                in1=c4_t[u][:, x * T4:(x + 1) * T4].unsqueeze(2).to_broadcast([P, T4, DH]),
-                op=ALU.mult,
-            )
+            for t in range(T4):
+                nc.vector.tensor_scalar(
+                    out=a[:, t, :],
+                    in0=v_sb[u][:, x, t * DH:(t + 1) * DH],
+                    scalar1=c4_t[u][:, x * T4 + t:x * T4 + t + 1],
+                    scalar2=None,
+                    op0=ALU.mult,
+                )
             a_t[b] = a
 
         def st_AT(b):

@@ -22,7 +22,7 @@ NP = B // 2
 PRE = 4
 REP = 4
 WARM0 = 4
-WARM_STEPS = 2
+TARGET = 1280
 SCALE = math.sqrt(128.0)
 FLOPS = 2 * B * H * N * N * DH + 2 * B * N * (H * DH) * D
 
@@ -40,7 +40,8 @@ def tile_attn_pb_t_kernel(tc, q_rot, k_rot, v, w_out, b_out, out):
         mxp = ctx.enter_context(tc.tile_pool(name="mxp", bufs=3))
         outp = ctx.enter_context(tc.tile_pool(name="outp", bufs=3))
         ps_t = ctx.enter_context(tc.psum_pool(name="ps_t", bufs=2))
-        ps_s = ctx.enter_context(tc.psum_pool(name="ps_s", bufs=3))
+        ps_s = ctx.enter_context(tc.psum_pool(name="ps_s", bufs=2))
+        ps_d = ctx.enter_context(tc.psum_pool(name="ps_d", bufs=1))
         ps_c = ctx.enter_context(tc.psum_pool(name="ps_c", bufs=1))
         ps_x = ctx.enter_context(tc.psum_pool(name="ps_x", bufs=1))
         ps_o = ctx.enter_context(tc.psum_pool(name="ps_o", bufs=1))
@@ -68,9 +69,9 @@ def tile_attn_pb_t_kernel(tc, q_rot, k_rot, v, w_out, b_out, out):
 
         def warm(n):
             for x in range(n):
-                dm = ps_o.tile([P, 2, D], F32, name="po")
+                dm = ps_d.tile([P, 2 * D], F32, name="dm")
                 nc.tensor.matmul_mx(
-                    out=dm[:].rearrange("p b d -> p (b d)"),
+                    out=dm[:],
                     lhsT=zcod[:, 0:P].bitcast(FP8X4),
                     lhsT_scale=zscl[:, 0:P],
                     rhs=zcod[:].bitcast(FP8X4),
@@ -133,10 +134,8 @@ def tile_attn_pb_t_kernel(tc, q_rot, k_rot, v, w_out, b_out, out):
             nm_t[b] = nm
 
         def st_EXP(b):
-            u, x = divmod(b, 2)
             e = work.tile([P, T4, H, J], F32, name="e")
-            if x == 0:
-                z_t[u] = small.tile([P, 2 * H], F32, name="z")
+            z = small.tile([P, H], F32, name="z")
             for h in range(H):
                 nc.scalar.activation(
                     out=e[:, :, h, :],
@@ -144,14 +143,15 @@ def tile_attn_pb_t_kernel(tc, q_rot, k_rot, v, w_out, b_out, out):
                     func=ACTF.Exp,
                     bias=nm_t[b][:, h:h + 1],
                     scale=SCALE,
-                    accum_out=z_t[u][:, x * H + h:x * H + h + 1],
+                    accum_out=z[:, h:h + 1],
                 )
             e_t[b] = e
+            z_t[b] = z
 
-        def st_REC(u):
-            r = small.tile([P, 2 * H], F32, name="r")
-            nc.vector.reciprocal(out=r[:], in_=z_t[u][:])
-            r_t[u] = r
+        def st_REC(b):
+            r = small.tile([P, H], F32, name="r")
+            nc.vector.reciprocal(out=r[:], in_=z_t[b][:])
+            r_t[b] = r
 
         def st_C(b):
             u, x = divmod(b, 2)
@@ -161,7 +161,7 @@ def tile_attn_pb_t_kernel(tc, q_rot, k_rot, v, w_out, b_out, out):
                 nc.tensor.matmul(
                     pc_t[u][:, x, t, :, :],
                     lhsT=e_t[b][:, t, :, :].rearrange("p h j -> p (h j)"),
-                    rhs=r_t[u][:, x * H:(x + 1) * H].unsqueeze(1).to_broadcast([P, REP, H]),
+                    rhs=r_t[b][:].unsqueeze(1).to_broadcast([P, REP, H]),
                     start=True,
                     stop=True,
                 )
@@ -201,10 +201,7 @@ def tile_attn_pb_t_kernel(tc, q_rot, k_rot, v, w_out, b_out, out):
         def st_XEV(u):
             grp = mxp.tile([P, 2 * N * H], BF16, name="grp", align_bytes=64)
             src = xt_t[u][:].rearrange("p b j t h -> p (b j t h)")
-            if u % 2 == 1:
-                nc.scalar.copy(out=grp[:], in_=src)
-            else:
-                nc.vector.tensor_copy(out=grp[:], in_=src)
+            nc.scalar.copy(out=grp[:], in_=src)
             grp_t[u] = grp
 
         def st_QZ(u):
@@ -234,42 +231,48 @@ def tile_attn_pb_t_kernel(tc, q_rot, k_rot, v, w_out, b_out, out):
             )
             nc.sync.dma_start(out=out[2 * u:2 * u + 2].rearrange("b m d -> m b d"), in_=o[:])
 
-        def ok(u):
-            return 0 <= u < NP
+        def ok(b):
+            return 0 <= b < B
 
-        for i in range(NP + 7):
-            if ok(i + PRE):
-                load(i + PRE)
-            if ok(i - 6):
-                st_QZ(i - 6)
-            if ok(i - 2):
-                st_REC(i - 2)
-            if i == 3:
+        def oku(x2):
+            return x2 % 2 == 0 and 0 <= x2 // 2 < NP
+
+        for k in range(B + 12):
+            if k % 2 == 0 and k // 2 + PRE < NP:
+                load(k // 2 + PRE)
+            if oku(k - 10):
+                st_QZ((k - 10) // 2)
+            if oku(k - 11):
+                st_OUT((k - 11) // 2)
+            if k == 6:
                 prep_w()
-            if ok(i - 5):
-                st_XEV(i - 5)
-            if ok(i):
-                for b in (2 * i, 2 * i + 1):
-                    st_T(b)
-                    st_EV(b)
-            if i < WARM_STEPS:
-                warm(2)
-            if ok(i - 1):
-                for b in (2 * i - 2, 2 * i - 1):
-                    st_QK(b)
-                    st_MAX(b)
-                    st_EXP(b)
-            for x in range(2):
-                if ok(i - 2):
-                    st_C(2 * (i - 2) + x)
-                if ok(i - 6):
-                    st_MX(i - 6, x)
-            if ok(i - 2):
-                st_SEL(i - 2)
-                st_MUL(2 * (i - 2))
-                st_MUL(2 * (i - 2) + 1)
-            if ok(i - 6):
-                st_OUT(i - 6)
-            if ok(i - 4):
-                st_AT(2 * (i - 4))
-                st_AT(2 * (i - 4) + 1)
+            if oku(k - 8):
+                st_XEV((k - 8) // 2)
+            counted = 0
+            if ok(k):
+                st_T(k)
+                st_EV(k)
+            if ok(k - 1):
+                st_QK(k - 1)
+                counted += H * N
+            if oku(k - 10):
+                st_MX((k - 10) // 2, 0)
+                st_MX((k - 10) // 2, 1)
+                counted += 2 * D
+            if ok(k - 3):
+                counted += T4 * 4 * REP * H
+            if k < B and counted < TARGET:
+                warm((TARGET - counted + 511) // 512)
+            if ok(k - 1):
+                st_MAX(k - 1)
+                st_EXP(k - 1)
+            if ok(k - 2):
+                st_REC(k - 2)
+            if ok(k - 3):
+                st_C(k - 3)
+            if oku(k - 4):
+                st_SEL((k - 4) // 2)
+            if ok(k - 4):
+                st_MUL(k - 4)
+            if ok(k - 6):
+                st_AT(k - 6)

@@ -114,10 +114,12 @@ def tile_attn_pb_t_kernel(tc, q_rot, k_rot, v, w_out, b_out, out):
 
         def st_EV(b):
             qkT = work.tile([P, 2, H, N], BF16, name="qkT")
-            nc.scalar.copy(
-                out=qkT[:].rearrange("p y h n -> p (y h n)"),
-                in_=tqk_t[b][:].rearrange("p y h t j -> p (y h t j)"),
-            )
+            dst = qkT[:].rearrange("p y h n -> p (y h n)")
+            src = tqk_t[b][:].rearrange("p y h t j -> p (y h t j)")
+            if b % 4 == 1:
+                nc.vector.tensor_copy(out=dst, in_=src)
+            else:
+                nc.scalar.copy(out=dst, in_=src)
             qkT_t[b] = qkT
 
         def st_QK(b):
@@ -130,7 +132,7 @@ def tile_attn_pb_t_kernel(tc, q_rot, k_rot, v, w_out, b_out, out):
             mx = small.tile([P, H], F32, name="mx")
             nc.vector.tensor_reduce(out=mx[:], in_=s_t[b][:], axis=AX.X, op=ALU.max)
             nm = small.tile([P, H], F32, name="nm")
-            nc.vector.tensor_scalar(out=nm[:], in0=mx[:], scalar1=-SCALE, scalar2=None, op0=ALU.mult)
+            nc.scalar.mul(out=nm[:], in_=mx[:], mul=-SCALE)
             nm_t[b] = nm
 
         def st_EXP(b):
@@ -182,13 +184,23 @@ def tile_attn_pb_t_kernel(tc, q_rot, k_rot, v, w_out, b_out, out):
             u, x = divmod(b, 2)
             a = apool.tile([P, T4, DH], BF16, name="a")
             for t in range(T4):
-                nc.vector.tensor_scalar(
-                    out=a[:, t, :],
-                    in0=v_sb[u][:, x, t * DH:(t + 1) * DH],
-                    scalar1=c4_t[u][:, x * T4 + t:x * T4 + t + 1],
-                    scalar2=None,
-                    op0=ALU.mult,
-                )
+                if t < 3:
+                    nc.gpsimd.tensor_scalar(
+                        out=a[:, t, :],
+                        in0=v_sb[u][:, x, t * DH:(t + 1) * DH],
+                        scalar1=c4_t[u][:, x * T4 + t:x * T4 + t + 1],
+                        scalar2=0.0,
+                        op0=ALU.mult,
+                        op1=ALU.add,
+                    )
+                else:
+                    nc.vector.tensor_scalar(
+                        out=a[:, t, :],
+                        in0=v_sb[u][:, x, t * DH:(t + 1) * DH],
+                        scalar1=c4_t[u][:, x * T4 + t:x * T4 + t + 1],
+                        scalar2=None,
+                        op0=ALU.mult,
+                    )
             a_t[b] = a
 
         def st_AT(b):
@@ -201,7 +213,7 @@ def tile_attn_pb_t_kernel(tc, q_rot, k_rot, v, w_out, b_out, out):
         def st_XEV(u):
             grp = mxp.tile([P, 2 * N * H], BF16, name="grp", align_bytes=64)
             src = xt_t[u][:].rearrange("p b j t h -> p (b j t h)")
-            nc.scalar.copy(out=grp[:], in_=src)
+            nc.vector.tensor_copy(out=grp[:], in_=src)
             grp_t[u] = grp
 
         def st_QZ(u):

@@ -21,7 +21,7 @@ J = 32
 NP = B // 2
 PRE = 4
 REP = 4
-WARM0 = 4
+WARM0 = 8
 TARGET = 1280
 SCALE = math.sqrt(128.0)
 FLOPS = 2 * B * H * N * N * DH + 2 * B * N * (H * DH) * D
@@ -33,21 +33,20 @@ def tile_attn_pb_t_kernel(tc, q_rot, k_rot, v, w_out, b_out, out):
         ctx.enter_context(tc.manual_schedule())
         const = ctx.enter_context(tc.tile_pool(name="const", bufs=1))
         qk_in = ctx.enter_context(tc.tile_pool(name="qk_in", bufs=PRE + 2))
-        v_in = ctx.enter_context(tc.tile_pool(name="v_in", bufs=PRE + 4))
+        v_in = ctx.enter_context(tc.tile_pool(name="v_in", bufs=PRE + 5))
         work = ctx.enter_context(tc.tile_pool(name="work", bufs=6))
         apool = ctx.enter_context(tc.tile_pool(name="apool", bufs=8))
         small = ctx.enter_context(tc.tile_pool(name="small", bufs=4))
         mxp = ctx.enter_context(tc.tile_pool(name="mxp", bufs=3))
         outp = ctx.enter_context(tc.tile_pool(name="outp", bufs=3))
         ps_t = ctx.enter_context(tc.psum_pool(name="ps_t", bufs=2))
-        ps_s = ctx.enter_context(tc.psum_pool(name="ps_s", bufs=2))
-        ps_d = ctx.enter_context(tc.psum_pool(name="ps_d", bufs=1))
+        ps_s = ctx.enter_context(tc.psum_pool(name="ps_s", bufs=3))
         ps_c = ctx.enter_context(tc.psum_pool(name="ps_c", bufs=1))
         ps_x = ctx.enter_context(tc.psum_pool(name="ps_x", bufs=1))
         ps_o = ctx.enter_context(tc.psum_pool(name="ps_o", bufs=1))
 
         q_sb, k_sb, v_sb = {}, {}, {}
-        tqk_t, qkT_t, s_t, nm_t, e_t, z_t, r_t = {}, {}, {}, {}, {}, {}, {}
+        tqk_t, qkT_t, s_t, nm_t, e_t, z_t, r_t, mx_t = {}, {}, {}, {}, {}, {}, {}, {}
         pc_t, c4_t, a_t, xt_t, grp_t, cod_t, scl_t, po_t = {}, {}, {}, {}, {}, {}, {}, {}
 
         def load(j):
@@ -67,15 +66,14 @@ def tile_attn_pb_t_kernel(tc, q_rot, k_rot, v, w_out, b_out, out):
         nc.vector.memset(zsrc[:].bitcast(I32), 0)
         nc.vector.quantize_mx(out=zcod[:].bitcast(FP8X4), scales=zscl[:], in_=zsrc[:])
 
-        def warm(n):
+        def warm(n, s):
             for x in range(n):
-                dm = ps_d.tile([P, 2 * D], F32, name="dm")
                 nc.tensor.matmul_mx(
-                    out=dm[:],
+                    out=s[:, 2:4, :].rearrange("p h n -> p (h n)"),
                     lhsT=zcod[:, 0:P].bitcast(FP8X4),
                     lhsT_scale=zscl[:, 0:P],
-                    rhs=zcod[:].bitcast(FP8X4),
-                    rhs_scale=zscl[:],
+                    rhs=zcod[:, 0:D].bitcast(FP8X4),
+                    rhs_scale=zscl[:, 0:D],
                     start=True,
                     stop=True,
                 )
@@ -86,7 +84,7 @@ def tile_attn_pb_t_kernel(tc, q_rot, k_rot, v, w_out, b_out, out):
         nc.vector.tensor_copy(out=perm[:], in_=ident[:].rearrange("p (h j) -> p j h", h=H))
         mask = const.tile([P, H], F32, name="mask")
         nc.vector.tensor_reduce(out=mask[:], in_=ident[:].rearrange("p (h j) -> p h j", h=H), axis=AX.X, op=ALU.add)
-        warm(WARM0)
+        warm(WARM0, ps_s.tile([P, H, N], F32, name="s"))
 
         w_raw = const.tile([P, H, D], BF16, name="w_raw")
         nc.sync.dma_start(out=w_raw[:], in_=w_out.rearrange("(h p) n -> p h n", p=P))
@@ -104,38 +102,39 @@ def tile_attn_pb_t_kernel(tc, q_rot, k_rot, v, w_out, b_out, out):
                 out=w_cod[:].bitcast(FP8X4), scales=w_scl[:], in_=w_grp[:].rearrange("p n h -> p (n h)")
             )
 
-        def st_T(b):
+        def st_T(b, pieces):
             u, x = divmod(b, 2)
-            tqk = ps_t.tile([P, 2, H, T4, J], BF16, name="tqk")
-            for y, src in enumerate((q_sb[u], k_sb[u])):
-                for t in range(T4):
-                    nc.tensor.transpose(tqk[:, y, :, t, :], src[:, x, t * DH:(t + 1) * DH], ident[:])
-            tqk_t[b] = tqk
+            if b not in tqk_t:
+                tqk_t[b] = ps_t.tile([P, 2, H, T4, J], BF16, name="tqk")
+            for i in pieces:
+                y, t = divmod(i, T4)
+                src = (q_sb[u], k_sb[u])[y]
+                nc.tensor.transpose(tqk_t[b][:, y, :, t, :], src[:, x, t * DH:(t + 1) * DH], ident[:])
 
         def st_EV(b):
             qkT = work.tile([P, 2, H, N], BF16, name="qkT")
-            dst = qkT[:].rearrange("p y h n -> p (y h n)")
-            src = tqk_t[b][:].rearrange("p y h t j -> p (y h t j)")
-            if b % 4 == 1:
-                nc.vector.tensor_copy(out=dst, in_=src)
-            else:
-                nc.scalar.copy(out=dst, in_=src)
+            nc.scalar.copy(
+                out=qkT[:].rearrange("p y h n -> p (y h n)").bitcast(F32),
+                in_=tqk_t[b][:].rearrange("p y h t j -> p (y h t j)").bitcast(F32),
+            )
             qkT_t[b] = qkT
 
-        def st_QK(b):
-            s = ps_s.tile([P, H, N], F32, name="s")
-            for h in range(H):
+        def st_QK(b, hs):
+            if b not in s_t:
+                s_t[b] = ps_s.tile([P, H, N], F32, name="s")
+            s = s_t[b]
+            for h in hs:
                 nc.tensor.matmul(s[:, h, :], lhsT=qkT_t[b][:, 0, h, :], rhs=qkT_t[b][:, 1, h, :], start=True, stop=True)
-            s_t[b] = s
 
         def st_MAX(b):
             mx = small.tile([P, H], F32, name="mx")
             nc.vector.tensor_reduce(out=mx[:], in_=s_t[b][:], axis=AX.X, op=ALU.max)
-            nm = small.tile([P, H], F32, name="nm")
-            nc.scalar.mul(out=nm[:], in_=mx[:], mul=-SCALE)
-            nm_t[b] = nm
+            mx_t[b] = mx
 
         def st_EXP(b):
+            nm = small.tile([P, H], F32, name="nm")
+            nc.scalar.mul(out=nm[:], in_=mx_t[b][:], mul=-SCALE)
+            nm_t[b] = nm
             e = work.tile([P, T4, H, J], F32, name="e")
             z = small.tile([P, H], F32, name="z")
             for h in range(H):
@@ -155,11 +154,11 @@ def tile_attn_pb_t_kernel(tc, q_rot, k_rot, v, w_out, b_out, out):
             nc.vector.reciprocal(out=r[:], in_=z_t[b][:])
             r_t[b] = r
 
-        def st_C(b):
+        def st_C(b, ts):
             u, x = divmod(b, 2)
-            if x == 0:
+            if u not in pc_t:
                 pc_t[u] = ps_c.tile([P, 2, T4, REP, H], F32, name="pc")
-            for t in range(T4):
+            for t in ts:
                 nc.tensor.matmul(
                     pc_t[u][:, x, t, :, :],
                     lhsT=e_t[b][:, t, :, :].rearrange("p h j -> p (h j)"),
@@ -184,7 +183,7 @@ def tile_attn_pb_t_kernel(tc, q_rot, k_rot, v, w_out, b_out, out):
             u, x = divmod(b, 2)
             a = apool.tile([P, T4, DH], BF16, name="a")
             for t in range(T4):
-                if t < 3:
+                if t < 2:
                     nc.gpsimd.tensor_scalar(
                         out=a[:, t, :],
                         in0=v_sb[u][:, x, t * DH:(t + 1) * DH],
@@ -203,11 +202,11 @@ def tile_attn_pb_t_kernel(tc, q_rot, k_rot, v, w_out, b_out, out):
                     )
             a_t[b] = a
 
-        def st_AT(b):
+        def st_AT(b, ts):
             u, x = divmod(b, 2)
-            if x == 0:
+            if u not in xt_t:
                 xt_t[u] = ps_x.tile([P, 2, J, T4, H], BF16, name="xt")
-            for t in range(T4):
+            for t in ts:
                 nc.tensor.transpose(xt_t[u][:, x, :, t, :], a_t[b][:, t, :], perm[:].rearrange("p j h -> p (j h)"))
 
         def st_XEV(u):
@@ -249,42 +248,53 @@ def tile_attn_pb_t_kernel(tc, q_rot, k_rot, v, w_out, b_out, out):
         def oku(x2):
             return x2 % 2 == 0 and 0 <= x2 // 2 < NP
 
-        for k in range(B + 12):
+        for k in range(B + 11):
             if k % 2 == 0 and k // 2 + PRE < NP:
                 load(k // 2 + PRE)
-            if oku(k - 10):
-                st_QZ((k - 10) // 2)
-            if oku(k - 11):
-                st_OUT((k - 11) // 2)
-            if k == 6:
+            if oku(k - 6):
+                st_SEL((k - 6) // 2)
+                st_MUL(k - 6)
+                st_MUL(k - 5)
+            if ok(k - 2):
+                st_MAX(k - 2)
+            if oku(k - 12):
+                st_OUT((k - 12) // 2)
+            if oku(k - 9):
+                st_XEV((k - 9) // 2)
+            if k == 8:
                 prep_w()
-            if oku(k - 8):
-                st_XEV((k - 8) // 2)
+            if ok(k - 3):
+                st_EXP(k - 3)
+                st_REC(k - 3)
+            if oku(k - 9):
+                st_QZ((k - 9) // 2)
             counted = 0
             if ok(k):
-                st_T(k)
+                st_T(k, (0, 1, 2))
+            if ok(k - 1):
+                st_QK(k - 1, (0,))
+                counted += H * N
+            if ok(k):
+                st_T(k, (3, 4, 5))
+            if ok(k - 1):
+                st_QK(k - 1, (1,))
+            if oku(k - 11):
+                st_MX((k - 11) // 2, 0)
+                st_MX((k - 11) // 2, 1)
+                counted += 2 * D
+            if ok(k - 4):
+                counted += T4 * 4 * REP * H
+            if ok(k - 1) and counted < TARGET:
+                warm((TARGET - counted + D - 1) // D, s_t[k - 1])
+            if ok(k - 1):
+                st_QK(k - 1, (2,))
+            if ok(k):
+                st_T(k, (6, 7))
                 st_EV(k)
             if ok(k - 1):
-                st_QK(k - 1)
-                counted += H * N
-            if oku(k - 10):
-                st_MX((k - 10) // 2, 0)
-                st_MX((k - 10) // 2, 1)
-                counted += 2 * D
-            if ok(k - 3):
-                counted += T4 * 4 * REP * H
-            if k < B and counted < TARGET:
-                warm((TARGET - counted + 511) // 512)
-            if ok(k - 1):
-                st_MAX(k - 1)
-                st_EXP(k - 1)
-            if ok(k - 2):
-                st_REC(k - 2)
-            if ok(k - 3):
-                st_C(k - 3)
-            if oku(k - 4):
-                st_SEL((k - 4) // 2)
-            if ok(k - 4):
-                st_MUL(k - 4)
-            if ok(k - 6):
-                st_AT(k - 6)
+                st_QK(k - 1, (3,))
+            for t in range(T4):
+                if ok(k - 4):
+                    st_C(k - 4, (t,))
+                if ok(k - 7):
+                    st_AT(k - 7, (t,))

@@ -20,9 +20,9 @@ T4 = 4
 J = 32
 NP = B // 2
 PRE = 4
-REP = 4
+REP = 5
 WARM0 = 8
-TARGET = 1280
+TARGET = 1024
 SCALE = math.sqrt(128.0)
 FLOPS = 2 * B * H * N * N * DH + 2 * B * N * (H * DH) * D
 
@@ -102,14 +102,13 @@ def tile_attn_pb_t_kernel(tc, q_rot, k_rot, v, w_out, b_out, out):
                 out=w_cod[:].bitcast(FP8X4), scales=w_scl[:], in_=w_grp[:].rearrange("p n h -> p (n h)")
             )
 
-        def st_T(b, pieces):
+        def st_T(b):
             u, x = divmod(b, 2)
-            if b not in tqk_t:
-                tqk_t[b] = ps_t.tile([P, 2, H, T4, J], BF16, name="tqk")
-            for i in pieces:
-                y, t = divmod(i, T4)
-                src = (q_sb[u], k_sb[u])[y]
-                nc.tensor.transpose(tqk_t[b][:, y, :, t, :], src[:, x, t * DH:(t + 1) * DH], ident[:])
+            tqk = ps_t.tile([P, 2, H, T4, J], BF16, name="tqk")
+            for y, src in enumerate((q_sb[u], k_sb[u])):
+                for t in range(T4):
+                    nc.tensor.transpose(tqk[:, y, :, t, :], src[:, x, t * DH:(t + 1) * DH], ident[:])
+            tqk_t[b] = tqk
 
         def st_EV(b):
             qkT = work.tile([P, 2, H, N], BF16, name="qkT")
@@ -202,11 +201,11 @@ def tile_attn_pb_t_kernel(tc, q_rot, k_rot, v, w_out, b_out, out):
                     )
             a_t[b] = a
 
-        def st_AT(b, ts):
+        def st_AT(b):
             u, x = divmod(b, 2)
-            if u not in xt_t:
+            if x == 0:
                 xt_t[u] = ps_x.tile([P, 2, J, T4, H], BF16, name="xt")
-            for t in ts:
+            for t in range(T4):
                 nc.tensor.transpose(xt_t[u][:, x, :, t, :], a_t[b][:, t, :], perm[:].rearrange("p j h -> p (j h)"))
 
         def st_XEV(u):
@@ -248,17 +247,17 @@ def tile_attn_pb_t_kernel(tc, q_rot, k_rot, v, w_out, b_out, out):
         def oku(x2):
             return x2 % 2 == 0 and 0 <= x2 // 2 < NP
 
-        for k in range(B + 11):
+        for k in range(B + 12):
             if k % 2 == 0 and k // 2 + PRE < NP:
                 load(k // 2 + PRE)
             if oku(k - 6):
                 st_SEL((k - 6) // 2)
                 st_MUL(k - 6)
                 st_MUL(k - 5)
+            if oku(k - 13):
+                st_OUT((k - 13) // 2)
             if ok(k - 2):
                 st_MAX(k - 2)
-            if oku(k - 12):
-                st_OUT((k - 12) // 2)
             if oku(k - 9):
                 st_XEV((k - 9) // 2)
             if k == 8:
@@ -268,33 +267,26 @@ def tile_attn_pb_t_kernel(tc, q_rot, k_rot, v, w_out, b_out, out):
                 st_REC(k - 3)
             if oku(k - 9):
                 st_QZ((k - 9) // 2)
+            if ok(k):
+                st_T(k)
+                st_EV(k)
             counted = 0
-            if ok(k):
-                st_T(k, (0, 1, 2))
             if ok(k - 1):
-                st_QK(k - 1, (0,))
+                st_QK(k - 1, (0, 1))
                 counted += H * N
-            if ok(k):
-                st_T(k, (3, 4, 5))
-            if ok(k - 1):
-                st_QK(k - 1, (1,))
-            if oku(k - 11):
-                st_MX((k - 11) // 2, 0)
-                st_MX((k - 11) // 2, 1)
-                counted += 2 * D
+            if ok(k - 11):
+                counted += D
             if ok(k - 4):
                 counted += T4 * 4 * REP * H
             if ok(k - 1) and counted < TARGET:
                 warm((TARGET - counted + D - 1) // D, s_t[k - 1])
             if ok(k - 1):
-                st_QK(k - 1, (2,))
-            if ok(k):
-                st_T(k, (6, 7))
-                st_EV(k)
-            if ok(k - 1):
-                st_QK(k - 1, (3,))
-            for t in range(T4):
-                if ok(k - 4):
-                    st_C(k - 4, (t,))
-                if ok(k - 7):
-                    st_AT(k - 7, (t,))
+                st_QK(k - 1, (2, 3))
+            if ok(k - 4):
+                st_C(k - 4, (0, 1))
+            if ok(k - 11):
+                st_MX((k - 11) // 2, (k - 11) % 2)
+            if ok(k - 4):
+                st_C(k - 4, (2, 3))
+            if ok(k - 7):
+                st_AT(k - 7)

@@ -20,9 +20,12 @@ T4 = 4
 J = 32
 NP = B // 2
 PRE = 4
-REP = 5
-WARM0 = 8
+XS = 3
+NCF = 36
+NC = max(NCF, 8)
 TARGET = 1024
+MULP = 2
+WARM0 = 8
 SCALE = math.sqrt(128.0)
 FLOPS = 2 * B * H * N * N * DH + 2 * B * N * (H * DH) * D
 
@@ -33,10 +36,10 @@ def tile_attn_pb_t_kernel(tc, q_rot, k_rot, v, w_out, b_out, out):
         ctx.enter_context(tc.manual_schedule())
         const = ctx.enter_context(tc.tile_pool(name="const", bufs=1))
         qk_in = ctx.enter_context(tc.tile_pool(name="qk_in", bufs=PRE + 2))
-        v_in = ctx.enter_context(tc.tile_pool(name="v_in", bufs=PRE + 5))
-        work = ctx.enter_context(tc.tile_pool(name="work", bufs=6))
-        apool = ctx.enter_context(tc.tile_pool(name="apool", bufs=8))
-        small = ctx.enter_context(tc.tile_pool(name="small", bufs=4))
+        v_in = ctx.enter_context(tc.tile_pool(name="v_in", bufs=PRE + 6))
+        work = ctx.enter_context(tc.tile_pool(name="work", bufs=8))
+        apool = ctx.enter_context(tc.tile_pool(name="apool", bufs=10))
+        small = ctx.enter_context(tc.tile_pool(name="small", bufs=6))
         mxp = ctx.enter_context(tc.tile_pool(name="mxp", bufs=3))
         outp = ctx.enter_context(tc.tile_pool(name="outp", bufs=3))
         ps_t = ctx.enter_context(tc.psum_pool(name="ps_t", bufs=2))
@@ -46,8 +49,8 @@ def tile_attn_pb_t_kernel(tc, q_rot, k_rot, v, w_out, b_out, out):
         ps_o = ctx.enter_context(tc.psum_pool(name="ps_o", bufs=1))
 
         q_sb, k_sb, v_sb = {}, {}, {}
-        tqk_t, qkT_t, s_t, nm_t, e_t, z_t, r_t, mx_t = {}, {}, {}, {}, {}, {}, {}, {}
-        pc_t, c4_t, a_t, xt_t, grp_t, cod_t, scl_t, po_t = {}, {}, {}, {}, {}, {}, {}, {}
+        tqk_t, qkT_t, s_t, nm_t, e_t, z_t, r_t, rb_t, lo_t, mx_t = {}, {}, {}, {}, {}, {}, {}, {}, {}, {}
+        pc_t, tmp_t, c4_t, a_t, xt_t, grp_t, cod_t, scl_t, po_t = {}, {}, {}, {}, {}, {}, {}, {}, {}
 
         def load(j):
             for store, src, pool, nm in ((q_sb, q_rot, qk_in, "q"), (k_sb, k_rot, qk_in, "k"), (v_sb, v, v_in, "v")):
@@ -60,9 +63,9 @@ def tile_attn_pb_t_kernel(tc, q_rot, k_rot, v, w_out, b_out, out):
 
         for j in range(PRE):
             load(j)
-        zsrc = const.tile([P, 2048], BF16, name="zsrc", align_bytes=64)
-        zcod = const.tile([P, 512], U32, name="zcod", align_bytes=64)
-        zscl = const.tile([P, 512], U8, name="zscl", align_bytes=64)
+        zsrc = const.tile([P, 1024], BF16, name="zsrc", align_bytes=64)
+        zcod = const.tile([P, 256], U32, name="zcod", align_bytes=64)
+        zscl = const.tile([P, 256], U8, name="zscl", align_bytes=64)
         nc.vector.memset(zsrc[:].bitcast(I32), 0)
         nc.vector.quantize_mx(out=zcod[:].bitcast(FP8X4), scales=zscl[:], in_=zsrc[:])
 
@@ -84,6 +87,12 @@ def tile_attn_pb_t_kernel(tc, q_rot, k_rot, v, w_out, b_out, out):
         nc.vector.tensor_copy(out=perm[:], in_=ident[:].rearrange("p (h j) -> p j h", h=H))
         mask = const.tile([P, H], F32, name="mask")
         nc.vector.tensor_reduce(out=mask[:], in_=ident[:].rearrange("p (h j) -> p h j", h=H), axis=AX.X, op=ALU.add)
+        maskf = const.tile([P, 2, T4, 2, H], F32, name="maskf")
+        nc.vector.memset(maskf[:], 0.0)
+        for x in range(2):
+            for t in range(T4):
+                for a in range(2 if t < XS else 1):
+                    nc.vector.tensor_copy(out=maskf[:, x, t, a, :], in_=mask[:])
         warm(WARM0, ps_s.tile([P, H, N], F32, name="s"))
 
         w_raw = const.tile([P, H, D], BF16, name="w_raw")
@@ -118,11 +127,14 @@ def tile_attn_pb_t_kernel(tc, q_rot, k_rot, v, w_out, b_out, out):
             )
             qkT_t[b] = qkT
 
-        def st_QK(b, hs):
-            if b not in s_t:
-                s_t[b] = ps_s.tile([P, H, N], F32, name="s")
-            s = s_t[b]
-            for h in hs:
+        fill_n = {}
+
+        def st_QK(b):
+            s = ps_s.tile([P, H, N], F32, name="s")
+            s_t[b] = s
+            for h in range(H):
+                if h == 2:
+                    warm(fill_n[b], s)
                 nc.tensor.matmul(s[:, h, :], lhsT=qkT_t[b][:, 0, h, :], rhs=qkT_t[b][:, 1, h, :], start=True, stop=True)
 
         def st_MAX(b):
@@ -130,12 +142,16 @@ def tile_attn_pb_t_kernel(tc, q_rot, k_rot, v, w_out, b_out, out):
             nc.vector.tensor_reduce(out=mx[:], in_=s_t[b][:], axis=AX.X, op=ALU.max)
             mx_t[b] = mx
 
-        def st_EXP(b):
+        def st_NM(b):
             nm = small.tile([P, H], F32, name="nm")
-            nc.scalar.mul(out=nm[:], in_=mx_t[b][:], mul=-SCALE)
+            nc.gpsimd.tensor_scalar(out=nm[:], in0=mx_t[b][:], scalar1=-SCALE, scalar2=0.0, op0=ALU.mult, op1=ALU.add)
             nm_t[b] = nm
+
+        def st_EXP(b):
+            u, x = divmod(b, 2)
             e = work.tile([P, T4, H, J], F32, name="e")
-            z = small.tile([P, H], F32, name="z")
+            if x == 0:
+                z_t[u] = small.tile([P, 2, H], F32, name="z")
             for h in range(H):
                 nc.scalar.activation(
                     out=e[:, :, h, :],
@@ -143,46 +159,74 @@ def tile_attn_pb_t_kernel(tc, q_rot, k_rot, v, w_out, b_out, out):
                     func=ACTF.Exp,
                     bias=nm_t[b][:, h:h + 1],
                     scale=SCALE,
-                    accum_out=z[:, h:h + 1],
+                    accum_out=z_t[u][:, x, h:h + 1],
                 )
             e_t[b] = e
-            z_t[b] = z
 
-        def st_REC(b):
-            r = small.tile([P, H], F32, name="r")
-            nc.vector.reciprocal(out=r[:], in_=z_t[b][:])
-            r_t[b] = r
+        def st_REC(u):
+            r = small.tile([P, 2, H], F32, name="r")
+            nc.vector.reciprocal(out=r[:], in_=z_t[u][:])
+            r_t[u] = r
+
+        def st_R1(u):
+            rb = small.tile([P, 2, 2, H], BF16, name="rb")
+            nc.vector.tensor_copy(out=rb[:, :, 0, :], in_=r_t[u][:])
+            rb_t[u] = rb
+
+        def st_R2(u):
+            nc.vector.tensor_tensor(out=rb_t[u][:, :, 1, :], in0=r_t[u][:], in1=rb_t[u][:, :, 0, :], op=ALU.subtract)
+
+        def hi_of(b):
+            return e_t[b][:].rearrange("p t h j -> p (t h j)").bitcast(BF16).rearrange("p (c two) -> p c two", two=2)[:, :, 1]
+
+        def st_LO(b):
+            lo = work.tile([P, XS * P], BF16, name="lo")
+            nc.vector.tensor_tensor(
+                out=lo[:],
+                in0=e_t[b][:].rearrange("p t h j -> p (t h j)")[:, 0:XS * P],
+                in1=hi_of(b)[:, 0:XS * P],
+                op=ALU.subtract,
+            )
+            lo_t[b] = lo
 
         def st_C(b, ts):
             u, x = divmod(b, 2)
             if u not in pc_t:
-                pc_t[u] = ps_c.tile([P, 2, T4, REP, H], F32, name="pc")
+                pc_t[u] = ps_c.tile([P, 2, T4, NC], F32, name="pc")
             for t in ts:
-                nc.tensor.matmul(
-                    pc_t[u][:, x, t, :, :],
-                    lhsT=e_t[b][:, t, :, :].rearrange("p h j -> p (h j)"),
-                    rhs=r_t[b][:].unsqueeze(1).to_broadcast([P, REP, H]),
-                    start=True,
-                    stop=True,
-                )
+                if t < XS:
+                    rhs = rb_t[u][:, x, :, :].rearrange("p a h -> p (a h)")
+                    nc.tensor.matmul(pc_t[u][:, x, t, 0:2 * H], lhsT=hi_of(b)[:, t * P:(t + 1) * P], rhs=rhs, start=True, stop=False)
+                    nc.tensor.matmul(pc_t[u][:, x, t, 0:2 * H], lhsT=lo_t[b][:, t * P:(t + 1) * P], rhs=rhs, start=False, stop=True)
+                else:
+                    nc.tensor.matmul(
+                        pc_t[u][:, x, t, 0:NCF].rearrange("p (a h) -> p a h", h=H),
+                        lhsT=e_t[b][:, t, :, :].rearrange("p h j -> p (h j)"),
+                        rhs=r_t[u][:, x, :].unsqueeze(1).to_broadcast([P, NCF // H, H]),
+                        start=True,
+                        stop=True,
+                    )
 
-        def st_SEL(u):
-            tmp = small.tile([P, 2 * T4, H], F32, name="tmp")
+        def st_SELa(u):
+            tmp = small.tile([P, 2 * T4, 2 * H], F32, name="tmp")
             nc.vector.tensor_tensor(
                 out=tmp[:],
-                in0=pc_t[u][:, :, :, 0, :].rearrange("p b t h -> p (b t) h"),
-                in1=mask[:].unsqueeze(1).to_broadcast([P, 2 * T4, H]),
+                in0=pc_t[u][:, :, :, 0:2 * H].rearrange("p b t c -> p (b t) c"),
+                in1=maskf[:].rearrange("p b t a h -> p (b t) (a h)"),
                 op=ALU.mult,
             )
+            tmp_t[u] = tmp
+
+        def st_SELb(u):
             c4 = small.tile([P, 2 * T4], F32, name="c4")
-            nc.vector.tensor_reduce(out=c4[:], in_=tmp[:], axis=AX.X, op=ALU.add)
+            nc.vector.tensor_reduce(out=c4[:], in_=tmp_t[u][:], axis=AX.X, op=ALU.add)
             c4_t[u] = c4
 
         def st_MUL(b):
             u, x = divmod(b, 2)
             a = apool.tile([P, T4, DH], BF16, name="a")
             for t in range(T4):
-                if t < 2:
+                if t < MULP:
                     nc.gpsimd.tensor_scalar(
                         out=a[:, t, :],
                         in0=v_sb[u][:, x, t * DH:(t + 1) * DH],
@@ -211,7 +255,7 @@ def tile_attn_pb_t_kernel(tc, q_rot, k_rot, v, w_out, b_out, out):
         def st_XEV(u):
             grp = mxp.tile([P, 2 * N * H], BF16, name="grp", align_bytes=64)
             src = xt_t[u][:].rearrange("p b j t h -> p (b j t h)")
-            nc.vector.tensor_copy(out=grp[:], in_=src)
+            nc.scalar.copy(out=grp[:].bitcast(F32), in_=src.bitcast(F32))
             grp_t[u] = grp
 
         def st_QZ(u):
@@ -221,7 +265,8 @@ def tile_attn_pb_t_kernel(tc, q_rot, k_rot, v, w_out, b_out, out):
             cod_t[u] = cod
             scl_t[u] = scl
 
-        def st_MX(u, x):
+        def st_MX(b):
+            u, x = divmod(b, 2)
             if x == 0:
                 po_t[u] = ps_o.tile([P, 2, D], F32, name="po")
             nc.tensor.matmul_mx(
@@ -241,52 +286,56 @@ def tile_attn_pb_t_kernel(tc, q_rot, k_rot, v, w_out, b_out, out):
             )
             nc.sync.dma_start(out=out[2 * u:2 * u + 2].rearrange("b m d -> m b d"), in_=o[:])
 
-        def ok(b):
-            return 0 <= b < B
+        def st_C0(b):
+            st_C(b, (0, 1))
 
-        def oku(x2):
-            return x2 % 2 == 0 and 0 <= x2 // 2 < NP
+        def st_C1(b):
+            st_C(b, (2, 3))
 
-        for k in range(B + 12):
+        order = (
+            (st_SELa, 7, True),
+            (st_REC, 4, True),
+            (st_OUT, 14, True),
+            (st_SELb, 7, True),
+            (st_R1, 4, True),
+            (st_MAX, 2, False),
+            (st_R2, 4, True),
+            (st_NM, 2, False),
+            (st_MUL, 8, False),
+            (st_LO, 4, False),
+            (st_QZ, 11, True),
+            (st_EXP, 3, False),
+            (st_XEV, 10, True),
+            (st_T, 0, False),
+            (st_EV, 0, False),
+            (st_QK, 1, False),
+            (st_C0, 6, False),
+            (st_MX, 13, False),
+            (st_C1, 6, False),
+            (st_AT, 9, False),
+        )
+        last = max(lag for st, lag, pair in order)
+        for k in range(B + last + 1):
             if k % 2 == 0 and k // 2 + PRE < NP:
                 load(k // 2 + PRE)
-            if oku(k - 6):
-                st_SEL((k - 6) // 2)
-                st_MUL(k - 6)
-                st_MUL(k - 5)
-            if oku(k - 13):
-                st_OUT((k - 13) // 2)
-            if ok(k - 2):
-                st_MAX(k - 2)
-            if oku(k - 9):
-                st_XEV((k - 9) // 2)
             if k == 8:
                 prep_w()
-            if ok(k - 3):
-                st_EXP(k - 3)
-                st_REC(k - 3)
-            if oku(k - 9):
-                st_QZ((k - 9) // 2)
-            if ok(k):
-                st_T(k)
-                st_EV(k)
             counted = 0
-            if ok(k - 1):
-                st_QK(k - 1, (0, 1))
-                counted += H * N
-            if ok(k - 11):
-                counted += D
-            if ok(k - 4):
-                counted += T4 * 4 * REP * H
-            if ok(k - 1) and counted < TARGET:
-                warm((TARGET - counted + D - 1) // D, s_t[k - 1])
-            if ok(k - 1):
-                st_QK(k - 1, (2, 3))
-            if ok(k - 4):
-                st_C(k - 4, (0, 1))
-            if ok(k - 11):
-                st_MX((k - 11) // 2, (k - 11) % 2)
-            if ok(k - 4):
-                st_C(k - 4, (2, 3))
-            if ok(k - 7):
-                st_AT(k - 7)
+            for st, lag, pair in order:
+                if 0 <= k - lag < B:
+                    if st == st_QK:
+                        counted += H * N
+                    if st == st_MX:
+                        counted += D
+                    if st == st_C0:
+                        counted += XS * 2 * 2 * H + (T4 - XS) * 4 * NCF
+            for st, lag, pair in order:
+                if st == st_QK:
+                    fill_n[k - lag] = max(0, (TARGET - counted + D - 1) // D)
+            for st, lag, pair in order:
+                i = k - lag
+                if pair:
+                    if i % 2 == 1 and 0 <= i // 2 < NP:
+                        st(i // 2)
+                elif 0 <= i < B:
+                    st(i)

@@ -20,9 +20,9 @@ T4 = 4
 J = 32
 NP = B // 2
 PRE = 4
-XS = 3
-NCF = 36
-NC = max(NCF, 8)
+XS = 2
+NCF = (32, 28)
+NC = max(NCF + (8,))
 TARGET = 1024
 MULP = 2
 WARM0 = 8
@@ -197,12 +197,13 @@ def tile_attn_pb_t_kernel(tc, q_rot, k_rot, v, w_out, b_out, out):
                 if t < XS:
                     rhs = rb_t[u][:, x, :, :].rearrange("p a h -> p (a h)")
                     nc.tensor.matmul(pc_t[u][:, x, t, 0:2 * H], lhsT=hi_of(b)[:, t * P:(t + 1) * P], rhs=rhs, start=True, stop=False)
-                    nc.tensor.matmul(pc_t[u][:, x, t, 0:2 * H], lhsT=lo_t[b][:, t * P:(t + 1) * P], rhs=rhs, start=False, stop=True)
+                    nc.tensor.matmul(pc_t[u][:, x, t, 0:H], lhsT=lo_t[b][:, t * P:(t + 1) * P], rhs=rb_t[u][:, x, 0, :], start=False, stop=True)
                 else:
+                    ncf = NCF[t - XS]
                     nc.tensor.matmul(
-                        pc_t[u][:, x, t, 0:NCF].rearrange("p (a h) -> p a h", h=H),
+                        pc_t[u][:, x, t, 0:ncf].rearrange("p (a h) -> p a h", h=H),
                         lhsT=e_t[b][:, t, :, :].rearrange("p h j -> p (h j)"),
-                        rhs=r_t[u][:, x, :].unsqueeze(1).to_broadcast([P, NCF // H, H]),
+                        rhs=r_t[u][:, x, :].unsqueeze(1).to_broadcast([P, ncf // H, H]),
                         start=True,
                         stop=True,
                     )
@@ -328,7 +329,7 @@ def tile_attn_pb_t_kernel(tc, q_rot, k_rot, v, w_out, b_out, out):
                     if st == st_MX:
                         counted += D
                     if st == st_C0:
-                        counted += XS * 2 * 2 * H + (T4 - XS) * 4 * NCF
+                        counted += XS * 3 * H + 4 * sum(NCF)
             for st, lag, pair in order:
                 if st == st_QK:
                     fill_n[k - lag] = max(0, (TARGET - counted + D - 1) // D)

@@ -24,7 +24,7 @@ XS = 2
 NCF = (32, 28)
 NC = max(NCF + (8,))
 TARGET = 1024
-MULP = 2
+MULP = 0
 WARM0 = 8
 SCALE = math.sqrt(128.0)
 FLOPS = 2 * B * H * N * N * DH + 2 * B * N * (H * DH) * D
@@ -144,7 +144,7 @@ def tile_attn_pb_t_kernel(tc, q_rot, k_rot, v, w_out, b_out, out):
 
         def st_NM(b):
             nm = small.tile([P, H], F32, name="nm")
-            nc.gpsimd.tensor_scalar(out=nm[:], in0=mx_t[b][:], scalar1=-SCALE, scalar2=0.0, op0=ALU.mult, op1=ALU.add)
+            nc.scalar.mul(out=nm[:], in_=mx_t[b][:], mul=-SCALE)
             nm_t[b] = nm
 
         def st_EXP(b):
@@ -294,35 +294,51 @@ def tile_attn_pb_t_kernel(tc, q_rot, k_rot, v, w_out, b_out, out):
             st_C(b, (2, 3))
 
         order = (
-            (st_SELa, 7, True),
-            (st_REC, 4, True),
-            (st_OUT, 14, True),
-            (st_SELb, 7, True),
-            (st_R1, 4, True),
-            (st_MAX, 2, False),
-            (st_R2, 4, True),
-            (st_NM, 2, False),
-            (st_MUL, 8, False),
-            (st_LO, 4, False),
-            (st_QZ, 11, True),
-            (st_EXP, 3, False),
-            (st_XEV, 10, True),
-            (st_T, 0, False),
-            (st_EV, 0, False),
-            (st_QK, 1, False),
-            (st_C0, 6, False),
-            (st_MX, 13, False),
-            (st_C1, 6, False),
-            (st_AT, 9, False),
+            (
+                (st_SELa, 7, True),
+                (st_MAX, 2, False),
+                (st_LO, 4, False),
+                (st_SELb, 7, True),
+                (st_QZ, 11, True),
+                (st_MUL, 8, False),
+                (st_EXP, 3, False),
+                (st_NM, 2, False),
+                (st_T, 0, False),
+                (st_EV, 0, False),
+                (st_QK, 1, False),
+                (st_C0, 6, False),
+                (st_MX, 13, False),
+                (st_C1, 6, False),
+                (st_AT, 9, False),
+            ),
+            (
+                (st_OUT, 14, True),
+                (st_MAX, 2, False),
+                (st_REC, 4, True),
+                (st_LO, 4, False),
+                (st_R1, 4, True),
+                (st_MUL, 8, False),
+                (st_R2, 4, True),
+                (st_EXP, 3, False),
+                (st_XEV, 10, True),
+                (st_NM, 2, False),
+                (st_T, 0, False),
+                (st_EV, 0, False),
+                (st_QK, 1, False),
+                (st_C0, 6, False),
+                (st_MX, 13, False),
+                (st_C1, 6, False),
+                (st_AT, 9, False),
+            ),
         )
-        last = max(lag for st, lag, pair in order)
+        last = max(lag for half in order for st, lag, pair in half)
         for k in range(B + last + 1):
             if k % 2 == 0 and k // 2 + PRE < NP:
                 load(k // 2 + PRE)
             if k == 8:
                 prep_w()
             counted = 0
-            for st, lag, pair in order:
+            for st, lag, pair in order[k % 2]:
                 if 0 <= k - lag < B:
                     if st == st_QK:
                         counted += H * N
@@ -330,13 +346,14 @@ def tile_attn_pb_t_kernel(tc, q_rot, k_rot, v, w_out, b_out, out):
                         counted += D
                     if st == st_C0:
                         counted += XS * 3 * H + 4 * sum(NCF)
-            for st, lag, pair in order:
+            for st, lag, pair in order[k % 2]:
                 if st == st_QK:
                     fill_n[k - lag] = max(0, (TARGET - counted + D - 1) // D)
-            for st, lag, pair in order:
+            for st, lag, pair in order[k % 2]:
                 i = k - lag
                 if pair:
-                    if i % 2 == 1 and 0 <= i // 2 < NP:
+                    assert i % 2 == 1
+                    if 0 <= i // 2 < NP:
                         st(i // 2)
                 elif 0 <= i < B:
                     st(i)

@@ -21,11 +21,12 @@ J = 32
 NP = B // 2
 PRE = 4
 XS = 2
-NCF = (32, 28)
+NCF = (40, 40)
 NC = max(NCF + (8,))
 TARGET = 1024
 MULP = 0
 WARM0 = 8
+RFN = 6
 SCALE = math.sqrt(128.0)
 FLOPS = 2 * B * H * N * N * DH + 2 * B * N * (H * DH) * D
 
@@ -53,13 +54,16 @@ def tile_attn_pb_t_kernel(tc, q_rot, k_rot, v, w_out, b_out, out):
         pc_t, tmp_t, c4_t, a_t, xt_t, grp_t, cod_t, scl_t, po_t = {}, {}, {}, {}, {}, {}, {}, {}, {}
 
         def load(j):
-            for store, src, pool, nm in ((q_sb, q_rot, qk_in, "q"), (k_sb, k_rot, qk_in, "k"), (v_sb, v, v_in, "v")):
+            for store, src, pool, nm in ((q_sb, q_rot, qk_in, "q"), (k_sb, k_rot, qk_in, "k")):
                 t = pool.tile([P, 2, T4 * DH], BF16, name=nm + "_sb")
                 nc.sync.dma_start(
                     out=t[:],
                     in_=src[2 * j:2 * j + 2].rearrange("b h (j t) d -> (h j) b (t d)", t=T4),
                 )
                 store[j] = t
+            t = v_in.tile([P, 2 * H, DH], BF16, name="v_sb")
+            nc.sync.dma_start(out=t[:], in_=v[2 * j:2 * j + 2].rearrange("b h m d -> m (b h) d"))
+            v_sb[j] = t
 
         for j in range(PRE):
             load(j)
@@ -69,34 +73,35 @@ def tile_attn_pb_t_kernel(tc, q_rot, k_rot, v, w_out, b_out, out):
         nc.vector.memset(zsrc[:].bitcast(I32), 0)
         nc.vector.quantize_mx(out=zcod[:].bitcast(FP8X4), scales=zscl[:], in_=zsrc[:])
 
-        def warm(n, s):
-            for x in range(n):
+        def warm(cols, s):
+            widths = [D] * (cols // D)
+            if cols % D > N:
+                widths.append(D)
+            elif cols % D > 0:
+                widths.append(N)
+            for wd in widths:
                 nc.tensor.matmul_mx(
-                    out=s[:, 2:4, :].rearrange("p h n -> p (h n)"),
+                    out=s[:, 2:2 + wd // N, :].rearrange("p h n -> p (h n)"),
                     lhsT=zcod[:, 0:P].bitcast(FP8X4),
                     lhsT_scale=zscl[:, 0:P],
-                    rhs=zcod[:, 0:D].bitcast(FP8X4),
-                    rhs_scale=zscl[:, 0:D],
+                    rhs=zcod[:, 0:wd].bitcast(FP8X4),
+                    rhs_scale=zscl[:, 0:wd],
                     start=True,
                     stop=True,
                 )
 
         ident = const.tile([P, P], BF16, name="ident")
         make_identity(nc, ident[:])
-        perm = const.tile([P, J, H], BF16, name="perm")
-        nc.vector.tensor_copy(out=perm[:], in_=ident[:].rearrange("p (h j) -> p j h", h=H))
-        mask = const.tile([P, H], F32, name="mask")
-        nc.vector.tensor_reduce(out=mask[:], in_=ident[:].rearrange("p (h j) -> p h j", h=H), axis=AX.X, op=ALU.add)
-        maskf = const.tile([P, 2, T4, 2, H], F32, name="maskf")
-        nc.vector.memset(maskf[:], 0.0)
-        for x in range(2):
-            for t in range(T4):
-                for a in range(2 if t < XS else 1):
-                    nc.vector.tensor_copy(out=maskf[:, x, t, a, :], in_=mask[:])
-        warm(WARM0, ps_s.tile([P, H, N], F32, name="s"))
+        ident32 = const.tile([P, P], F32, name="ident32")
+        make_identity(nc, ident32[:])
+        rf = []
+        for i in range(RFN):
+            rf.append(const.tile([P, 2, H, 2], F32, name="rf%d" % i))
+            nc.vector.memset(rf[i][:], 0.0)
+        warm(WARM0 * D, ps_s.tile([P, H, N], F32, name="s"))
 
-        w_raw = const.tile([P, H, D], BF16, name="w_raw")
-        nc.sync.dma_start(out=w_raw[:], in_=w_out.rearrange("(h p) n -> p h n", p=P))
+        w_raw = const.tile([P, 2, 2 * D], BF16, name="w_raw")
+        nc.sync.dma_start(out=w_raw[:], in_=w_out.rearrange("(u p e) n -> p u (e n)", u=2, e=2))
         bias_bf = const.tile([P, D], BF16, name="bias_bf")
         nc.sync.dma_start(out=bias_bf[:], in_=b_out.partition_broadcast(P))
         w_grp = const.tile([P, D, H], BF16, name="w_grp", align_bytes=64)
@@ -105,7 +110,7 @@ def tile_attn_pb_t_kernel(tc, q_rot, k_rot, v, w_out, b_out, out):
         bias = const.tile([P, D], F32, name="bias")
 
         def prep_w():
-            nc.vector.tensor_copy(out=w_grp[:], in_=w_raw[:].rearrange("p h n -> p n h"))
+            nc.vector.tensor_copy(out=w_grp[:], in_=w_raw[:].rearrange("p u (e n) -> p n (u e)", e=2))
             nc.vector.tensor_copy(out=bias[:], in_=bias_bf[:])
             nc.vector.quantize_mx(
                 out=w_cod[:].bitcast(FP8X4), scales=w_scl[:], in_=w_grp[:].rearrange("p n h -> p (n h)")
@@ -149,13 +154,13 @@ def tile_attn_pb_t_kernel(tc, q_rot, k_rot, v, w_out, b_out, out):
 
         def st_EXP(b):
             u, x = divmod(b, 2)
-            e = work.tile([P, T4, H, J], F32, name="e")
+            e = work.tile([P, H, N], F32, name="e")
             if x == 0:
                 z_t[u] = small.tile([P, 2, H], F32, name="z")
             for h in range(H):
                 nc.scalar.activation(
-                    out=e[:, :, h, :],
-                    in_=s_t[b][:, h, :].rearrange("p (t j) -> p t j", t=T4),
+                    out=e[:, h, :].rearrange("p (j t) -> p j t", t=T4),
+                    in_=s_t[b][:, h, :].rearrange("p (t j) -> p j t", t=T4),
                     func=ACTF.Exp,
                     bias=nm_t[b][:, h:h + 1],
                     scale=SCALE,
@@ -164,26 +169,25 @@ def tile_attn_pb_t_kernel(tc, q_rot, k_rot, v, w_out, b_out, out):
             e_t[b] = e
 
         def st_REC(u):
-            r = small.tile([P, 2, H], F32, name="r")
-            nc.vector.reciprocal(out=r[:], in_=z_t[u][:])
-            r_t[u] = r
+            r_t[u] = rf[u % RFN]
+            nc.vector.reciprocal(out=r_t[u][:, :, :, 0], in_=z_t[u][:])
 
         def st_R1(u):
-            rb = small.tile([P, 2, 2, H], BF16, name="rb")
-            nc.vector.tensor_copy(out=rb[:, :, 0, :], in_=r_t[u][:])
+            rb = small.tile([P, 2, H, 2], BF16, name="rb")
+            nc.vector.tensor_copy(out=rb[:, :, :, 0], in_=r_t[u][:, :, :, 0])
             rb_t[u] = rb
 
         def st_R2(u):
-            nc.vector.tensor_tensor(out=rb_t[u][:, :, 1, :], in0=r_t[u][:], in1=rb_t[u][:, :, 0, :], op=ALU.subtract)
+            nc.vector.tensor_tensor(out=rb_t[u][:, :, :, 1], in0=r_t[u][:, :, :, 0], in1=rb_t[u][:, :, :, 0], op=ALU.subtract)
 
         def hi_of(b):
-            return e_t[b][:].rearrange("p t h j -> p (t h j)").bitcast(BF16).rearrange("p (c two) -> p c two", two=2)[:, :, 1]
+            return e_t[b][:].rearrange("p h m -> p (h m)").bitcast(BF16).rearrange("p (c two) -> p c two", two=2)[:, :, 1]
 
         def st_LO(b):
             lo = work.tile([P, XS * P], BF16, name="lo")
             nc.vector.tensor_tensor(
                 out=lo[:],
-                in0=e_t[b][:].rearrange("p t h j -> p (t h j)")[:, 0:XS * P],
+                in0=e_t[b][:].rearrange("p h m -> p (h m)")[:, 0:XS * P],
                 in1=hi_of(b)[:, 0:XS * P],
                 op=ALU.subtract,
             )
@@ -195,32 +199,21 @@ def tile_attn_pb_t_kernel(tc, q_rot, k_rot, v, w_out, b_out, out):
                 pc_t[u] = ps_c.tile([P, 2, T4, NC], F32, name="pc")
             for t in ts:
                 if t < XS:
-                    rhs = rb_t[u][:, x, :, :].rearrange("p a h -> p (a h)")
-                    nc.tensor.matmul(pc_t[u][:, x, t, 0:2 * H], lhsT=hi_of(b)[:, t * P:(t + 1) * P], rhs=rhs, start=True, stop=False)
-                    nc.tensor.matmul(pc_t[u][:, x, t, 0:H], lhsT=lo_t[b][:, t * P:(t + 1) * P], rhs=rb_t[u][:, x, 0, :], start=False, stop=True)
+                    nc.tensor.matmul(pc_t[u][:, x, t, 0:2], lhsT=hi_of(b)[:, t * P:(t + 1) * P], rhs=rb_t[u][:, x, t, :], start=True, stop=False)
+                    nc.tensor.matmul(pc_t[u][:, x, t, 0:1], lhsT=lo_t[b][:, t * P:(t + 1) * P], rhs=rb_t[u][:, x, t, 0:1], start=False, stop=True)
                 else:
                     ncf = NCF[t - XS]
                     nc.tensor.matmul(
-                        pc_t[u][:, x, t, 0:ncf].rearrange("p (a h) -> p a h", h=H),
-                        lhsT=e_t[b][:, t, :, :].rearrange("p h j -> p (h j)"),
-                        rhs=r_t[u][:, x, :].unsqueeze(1).to_broadcast([P, ncf // H, H]),
+                        pc_t[u][:, x, t, 0:ncf].rearrange("p (c a) -> p c a", a=2),
+                        lhsT=e_t[b][:, t, :],
+                        rhs=r_t[u][:, x, t, :].unsqueeze(1).to_broadcast([P, ncf // 2, 2]),
                         start=True,
                         stop=True,
                     )
 
-        def st_SELa(u):
-            tmp = small.tile([P, 2 * T4, 2 * H], F32, name="tmp")
-            nc.vector.tensor_tensor(
-                out=tmp[:],
-                in0=pc_t[u][:, :, :, 0:2 * H].rearrange("p b t c -> p (b t) c"),
-                in1=maskf[:].rearrange("p b t a h -> p (b t) (a h)"),
-                op=ALU.mult,
-            )
-            tmp_t[u] = tmp
-
         def st_SELb(u):
             c4 = small.tile([P, 2 * T4], F32, name="c4")
-            nc.vector.tensor_reduce(out=c4[:], in_=tmp_t[u][:], axis=AX.X, op=ALU.add)
+            nc.vector.tensor_reduce(out=c4[:], in_=pc_t[u][:, :, :, 0:2].rearrange("p b t c -> p (b t) c"), axis=AX.X, op=ALU.add)
             c4_t[u] = c4
 
         def st_MUL(b):
@@ -230,7 +223,7 @@ def tile_attn_pb_t_kernel(tc, q_rot, k_rot, v, w_out, b_out, out):
                 if t < MULP:
                     nc.gpsimd.tensor_scalar(
                         out=a[:, t, :],
-                        in0=v_sb[u][:, x, t * DH:(t + 1) * DH],
+                        in0=v_sb[u][:, x * H + t, :],
                         scalar1=c4_t[u][:, x * T4 + t:x * T4 + t + 1],
                         scalar2=0.0,
                         op0=ALU.mult,
@@ -239,7 +232,7 @@ def tile_attn_pb_t_kernel(tc, q_rot, k_rot, v, w_out, b_out, out):
                 else:
                     nc.vector.tensor_scalar(
                         out=a[:, t, :],
-                        in0=v_sb[u][:, x, t * DH:(t + 1) * DH],
+                        in0=v_sb[u][:, x * H + t, :],
                         scalar1=c4_t[u][:, x * T4 + t:x * T4 + t + 1],
                         scalar2=None,
                         op0=ALU.mult,
@@ -249,14 +242,17 @@ def tile_attn_pb_t_kernel(tc, q_rot, k_rot, v, w_out, b_out, out):
         def st_AT(b):
             u, x = divmod(b, 2)
             if x == 0:
-                xt_t[u] = ps_x.tile([P, 2, J, T4, H], BF16, name="xt")
-            for t in range(T4):
-                nc.tensor.transpose(xt_t[u][:, x, :, t, :], a_t[b][:, t, :], perm[:].rearrange("p j h -> p (j h)"))
+                xt_t[u] = ps_x.tile([P, 2, 2, N], F32, name="xt")
+            words = a_t[b][:].rearrange("p h d -> p (h d)").bitcast(F32)
+            for w2 in range(2):
+                nc.tensor.transpose(xt_t[u][:, x, w2, :], words[:, w2 * P:(w2 + 1) * P], ident32[:])
 
         def st_XEV(u):
             grp = mxp.tile([P, 2 * N * H], BF16, name="grp", align_bytes=64)
-            src = xt_t[u][:].rearrange("p b j t h -> p (b j t h)")
-            nc.scalar.copy(out=grp[:].bitcast(F32), in_=src.bitcast(F32))
+            nc.scalar.copy(
+                out=grp[:].bitcast(F32).rearrange("p (b m w) -> p b m w", b=2, w=2),
+                in_=xt_t[u][:].rearrange("p b w m -> p b m w"),
+            )
             grp_t[u] = grp
 
         def st_QZ(u):
@@ -295,7 +291,6 @@ def tile_attn_pb_t_kernel(tc, q_rot, k_rot, v, w_out, b_out, out):
 
         order = (
             (
-                (st_SELa, 7, True),
                 (st_MAX, 2, False),
                 (st_LO, 4, False),
                 (st_SELb, 7, True),
@@ -345,10 +340,10 @@ def tile_attn_pb_t_kernel(tc, q_rot, k_rot, v, w_out, b_out, out):
                     if st == st_MX:
                         counted += D
                     if st == st_C0:
-                        counted += XS * 3 * H + 4 * sum(NCF)
+                        counted += XS * 3 + 4 * sum(NCF)
             for st, lag, pair in order[k % 2]:
                 if st == st_QK:
-                    fill_n[k - lag] = max(0, (TARGET - counted + D - 1) // D)
+                    fill_n[k - lag] = max(0, TARGET - counted)
             for st, lag, pair in order[k % 2]:
                 i = k - lag
                 if pair:

@@ -41,8 +41,8 @@ def tile_attn_pb_t_kernel(tc, q_rot, k_rot, v, w_out, b_out, out):
         work = ctx.enter_context(tc.tile_pool(name="work", bufs=8))
         apool = ctx.enter_context(tc.tile_pool(name="apool", bufs=10))
         small = ctx.enter_context(tc.tile_pool(name="small", bufs=6))
-        mxp = ctx.enter_context(tc.tile_pool(name="mxp", bufs=3))
-        outp = ctx.enter_context(tc.tile_pool(name="outp", bufs=3))
+        mxp = ctx.enter_context(tc.tile_pool(name="mxp", bufs=5))
+        outp = ctx.enter_context(tc.tile_pool(name="outp", bufs=5))
         ps_t = ctx.enter_context(tc.psum_pool(name="ps_t", bufs=2))
         ps_s = ctx.enter_context(tc.psum_pool(name="ps_s", bufs=3))
         ps_c = ctx.enter_context(tc.psum_pool(name="ps_c", bufs=1))
@@ -115,6 +115,9 @@ def tile_attn_pb_t_kernel(tc, q_rot, k_rot, v, w_out, b_out, out):
             nc.vector.quantize_mx(
                 out=w_cod[:].bitcast(FP8X4), scales=w_scl[:], in_=w_grp[:].rearrange("p n h -> p (n h)")
             )
+
+        xt_all = ps_x.tile([P, 2, 2, N], F32, name="xt")
+        po_all = ps_o.tile([P, 2, D], F32, name="po")
 
         def st_T(b):
             u, x = divmod(b, 2)
@@ -241,47 +244,45 @@ def tile_attn_pb_t_kernel(tc, q_rot, k_rot, v, w_out, b_out, out):
 
         def st_AT(b):
             u, x = divmod(b, 2)
-            if x == 0:
-                xt_t[u] = ps_x.tile([P, 2, 2, N], F32, name="xt")
+            xt_t[b] = xt_all[:, x, :, :]
             words = a_t[b][:].rearrange("p h d -> p (h d)").bitcast(F32)
             for w2 in range(2):
-                nc.tensor.transpose(xt_t[u][:, x, w2, :], words[:, w2 * P:(w2 + 1) * P], ident32[:])
+                nc.tensor.transpose(xt_t[b][:, w2, :], words[:, w2 * P:(w2 + 1) * P], ident32[:])
 
-        def st_XEV(u):
-            grp = mxp.tile([P, 2 * N * H], BF16, name="grp", align_bytes=64)
+        def st_XEV(b):
+            u, x = divmod(b, 2)
+            grp = mxp.tile([P, N * H], BF16, name="grp", align_bytes=64)
             nc.scalar.copy(
-                out=grp[:].bitcast(F32).rearrange("p (b m w) -> p b m w", b=2, w=2),
-                in_=xt_t[u][:].rearrange("p b w m -> p b m w"),
+                out=grp[:].bitcast(F32).rearrange("p (m w) -> p m w", w=2),
+                in_=xt_t[b].rearrange("p w m -> p m w"),
             )
-            grp_t[u] = grp
+            grp_t[b] = grp
 
-        def st_QZ(u):
-            cod = mxp.tile([P, 2 * N], U32, name="cod", align_bytes=64)
-            scl = mxp.tile([P, 2 * N], U8, name="scl", align_bytes=64)
-            nc.vector.quantize_mx(out=cod[:].bitcast(FP8X4), scales=scl[:], in_=grp_t[u][:])
-            cod_t[u] = cod
-            scl_t[u] = scl
+        def st_QZ(b):
+            cod = mxp.tile([P, N], U32, name="cod", align_bytes=64)
+            scl = mxp.tile([P, N], U8, name="scl", align_bytes=64)
+            nc.vector.quantize_mx(out=cod[:].bitcast(FP8X4), scales=scl[:], in_=grp_t[b][:])
+            cod_t[b] = cod
+            scl_t[b] = scl
 
         def st_MX(b):
             u, x = divmod(b, 2)
-            if x == 0:
-                po_t[u] = ps_o.tile([P, 2, D], F32, name="po")
+            po_t[b] = po_all[:, x, :]
             nc.tensor.matmul_mx(
-                out=po_t[u][:, x, :],
-                lhsT=cod_t[u][:, x * N:(x + 1) * N].bitcast(FP8X4),
-                lhsT_scale=scl_t[u][:, x * N:(x + 1) * N],
+                out=po_t[b],
+                lhsT=cod_t[b][:].bitcast(FP8X4),
+                lhsT_scale=scl_t[b][:],
                 rhs=w_cod[:].bitcast(FP8X4),
                 rhs_scale=w_scl[:],
                 start=True,
                 stop=True,
             )
 
-        def st_OUT(u):
-            o = outp.tile([P, 2, D], F32, name="o")
-            nc.vector.tensor_tensor(
-                out=o[:], in0=po_t[u][:], in1=bias[:].unsqueeze(1).to_broadcast([P, 2, D]), op=ALU.add
-            )
-            nc.sync.dma_start(out=out[2 * u:2 * u + 2].rearrange("b m d -> m b d"), in_=o[:])
+        def st_OUT(b):
+            u, x = divmod(b, 2)
+            o = outp.tile([P, D], F32, name="o")
+            nc.vector.tensor_tensor(out=o[:], in0=po_t[b], in1=bias[:], op=ALU.add)
+            nc.sync.dma_start(out=out[b], in_=o[:])
 
         def st_C0(b):
             st_C(b, (0, 1))
@@ -291,37 +292,40 @@ def tile_attn_pb_t_kernel(tc, q_rot, k_rot, v, w_out, b_out, out):
 
         order = (
             (
+                (st_OUT, 13, False),
+                (st_SELb, 7, True),
                 (st_MAX, 2, False),
                 (st_LO, 4, False),
-                (st_SELb, 7, True),
-                (st_QZ, 11, True),
+                (st_QZ, 11, False),
                 (st_MUL, 8, False),
                 (st_EXP, 3, False),
+                (st_XEV, 10, False),
                 (st_NM, 2, False),
                 (st_T, 0, False),
                 (st_EV, 0, False),
                 (st_QK, 1, False),
                 (st_C0, 6, False),
-                (st_MX, 13, False),
+                (st_MX, 12, False),
                 (st_C1, 6, False),
                 (st_AT, 9, False),
             ),
             (
-                (st_OUT, 14, True),
+                (st_OUT, 13, False),
                 (st_MAX, 2, False),
                 (st_REC, 4, True),
                 (st_LO, 4, False),
                 (st_R1, 4, True),
-                (st_MUL, 8, False),
+                (st_QZ, 11, False),
                 (st_R2, 4, True),
+                (st_MUL, 8, False),
                 (st_EXP, 3, False),
-                (st_XEV, 10, True),
+                (st_XEV, 10, False),
                 (st_NM, 2, False),
                 (st_T, 0, False),
                 (st_EV, 0, False),
                 (st_QK, 1, False),
                 (st_C0, 6, False),
-                (st_MX, 13, False),
+                (st_MX, 12, False),
                 (st_C1, 6, False),
                 (st_AT, 9, False),
             ),

@@ -293,6 +293,7 @@ def tile_attn_pb_t_kernel(tc, q_rot, k_rot, v, w_out, b_out, out):
         order = (
             (
                 (st_OUT, 13, False),
+                (st_R2, 5, True),
                 (st_SELb, 7, True),
                 (st_MAX, 2, False),
                 (st_LO, 4, False),
@@ -316,7 +317,6 @@ def tile_attn_pb_t_kernel(tc, q_rot, k_rot, v, w_out, b_out, out):
                 (st_LO, 4, False),
                 (st_R1, 4, True),
                 (st_QZ, 11, False),
-                (st_R2, 4, True),
                 (st_MUL, 8, False),
                 (st_EXP, 3, False),
                 (st_XEV, 10, False),

from contextlib import ExitStack
import math

import concourse.mybir as mybir
from concourse.masks import make_identity

F32 = mybir.dt.float32
BF16 = mybir.dt.bfloat16
I32 = mybir.dt.int32
U32 = mybir.dt.uint32
U8 = mybir.dt.uint8
FP8X4 = mybir.dt.float8_e4m3fn_x4
ALU = mybir.AluOpType
ACTF = mybir.ActivationFunctionType
AX = mybir.AxisListType

B, H, N, DH, D = 64, 4, 128, 128, 256
P = 128
T4 = 4
J = 32
NP = B // 2
PRE = 4
XS = 2
NCF = (40, 40)
NC = max(NCF + (8,))
TARGET = 1024
MULP = 0
WARM0 = 8
RFN = 6
SCALE = math.sqrt(128.0)
FLOPS = 2 * B * H * N * N * DH + 2 * B * N * (H * DH) * D


def tile_attn_pb_t_kernel(tc, q_rot, k_rot, v, w_out, b_out, out):
    nc = tc.nc
    with ExitStack() as ctx:
        ctx.enter_context(tc.manual_schedule())
        const = ctx.enter_context(tc.tile_pool(name="const", bufs=1))
        qk_in = ctx.enter_context(tc.tile_pool(name="qk_in", bufs=PRE + 2))
        v_in = ctx.enter_context(tc.tile_pool(name="v_in", bufs=PRE + 6))
        work = ctx.enter_context(tc.tile_pool(name="work", bufs=8))
        apool = ctx.enter_context(tc.tile_pool(name="apool", bufs=10))
        small = ctx.enter_context(tc.tile_pool(name="small", bufs=6))
        mxp = ctx.enter_context(tc.tile_pool(name="mxp", bufs=5))
        outp = ctx.enter_context(tc.tile_pool(name="outp", bufs=5))
        ps_t = ctx.enter_context(tc.psum_pool(name="ps_t", bufs=2))
        ps_s = ctx.enter_context(tc.psum_pool(name="ps_s", bufs=3))
        ps_c = ctx.enter_context(tc.psum_pool(name="ps_c", bufs=1))
        ps_x = ctx.enter_context(tc.psum_pool(name="ps_x", bufs=1))
        ps_o = ctx.enter_context(tc.psum_pool(name="ps_o", bufs=1))

        q_sb, k_sb, v_sb = {}, {}, {}
        tqk_t, qkT_t, s_t, nm_t, e_t, z_t, r_t, rb_t, lo_t, mx_t = {}, {}, {}, {}, {}, {}, {}, {}, {}, {}
        pc_t, tmp_t, c4_t, a_t, xt_t, grp_t, cod_t, scl_t, po_t = {}, {}, {}, {}, {}, {}, {}, {}, {}

        def load(j):
            for store, src, pool, nm in ((q_sb, q_rot, qk_in, "q"), (k_sb, k_rot, qk_in, "k")):
                t = pool.tile([P, 2, T4 * DH], BF16, name=nm + "_sb")
                nc.sync.dma_start(
                    out=t[:],
                    in_=src[2 * j:2 * j + 2].rearrange("b h (j t) d -> (h j) b (t d)", t=T4),
                )
                store[j] = t
            t = v_in.tile([P, 2 * H, DH], BF16, name="v_sb")
            nc.sync.dma_start(out=t[:], in_=v[2 * j:2 * j + 2].rearrange("b h m d -> m (b h) d"))
            v_sb[j] = t

        for j in range(PRE):
            load(j)
        zsrc = const.tile([P, 1024], BF16, name="zsrc", align_bytes=64)
        zcod = const.tile([P, 256], U32, name="zcod", align_bytes=64)
        zscl = const.tile([P, 256], U8, name="zscl", align_bytes=64)
        nc.vector.memset(zsrc[:].bitcast(I32), 0)
        nc.vector.quantize_mx(out=zcod[:].bitcast(FP8X4), scales=zscl[:], in_=zsrc[:])

        def warm(cols, s):
            widths = [D] * (cols // D)
            if cols % D > N:
                widths.append(D)
            elif cols % D > 0:
                widths.append(N)
            for wd in widths:
                nc.tensor.matmul_mx(
                    out=s[:, 2:2 + wd // N, :].rearrange("p h n -> p (h n)"),
                    lhsT=zcod[:, 0:P].bitcast(FP8X4),
                    lhsT_scale=zscl[:, 0:P],
                    rhs=zcod[:, 0:wd].bitcast(FP8X4),
                    rhs_scale=zscl[:, 0:wd],
                    start=True,
                    stop=True,
                )

        ident = const.tile([P, P], BF16, name="ident")
        make_identity(nc, ident[:])
        ident32 = const.tile([P, P], F32, name="ident32")
        make_identity(nc, ident32[:])
        rf = []
        for i in range(RFN):
            rf.append(const.tile([P, 2, H, 2], F32, name="rf%d" % i))
            nc.vector.memset(rf[i][:], 0.0)
        warm(WARM0 * D, ps_s.tile([P, H, N], F32, name="s"))

        w_raw = const.tile([P, 2, 2 * D], BF16, name="w_raw")
        nc.sync.dma_start(out=w_raw[:], in_=w_out.rearrange("(u p e) n -> p u (e n)", u=2, e=2))
        bias_bf = const.tile([P, D], BF16, name="bias_bf")
        nc.sync.dma_start(out=bias_bf[:], in_=b_out.partition_broadcast(P))
        w_grp = const.tile([P, D, H], BF16, name="w_grp", align_bytes=64)
        w_cod = const.tile([P, D], U32, name="w_cod", align_bytes=64)
        w_scl = const.tile([P, D], U8, name="w_scl", align_bytes=64)
        bias = const.tile([P, D], F32, name="bias")

        def prep_w():
            nc.vector.tensor_copy(out=w_grp[:], in_=w_raw[:].rearrange("p u (e n) -> p n (u e)", e=2))
            nc.vector.tensor_copy(out=bias[:], in_=bias_bf[:])
            nc.vector.quantize_mx(
                out=w_cod[:].bitcast(FP8X4), scales=w_scl[:], in_=w_grp[:].rearrange("p n h -> p (n h)")
            )

        xt_all = ps_x.tile([P, 2, 2, N], F32, name="xt")
        po_all = ps_o.tile([P, 2, D], F32, name="po")

        def st_T(b):
            u, x = divmod(b, 2)
            tqk = ps_t.tile([P, 2, H, T4, J], BF16, name="tqk")
            for y, src in enumerate((q_sb[u], k_sb[u])):
                for t in range(T4):
                    nc.tensor.transpose(tqk[:, y, :, t, :], src[:, x, t * DH:(t + 1) * DH], ident[:])
            tqk_t[b] = tqk

        def st_EV(b):
            qkT = work.tile([P, 2, H, N], BF16, name="qkT")
            nc.scalar.copy(
                out=qkT[:].rearrange("p y h n -> p (y h n)").bitcast(F32),
                in_=tqk_t[b][:].rearrange("p y h t j -> p (y h t j)").bitcast(F32),
            )
            qkT_t[b] = qkT

        fill_n = {}

        def st_QK(b):
            s = ps_s.tile([P, H, N], F32, name="s")
            s_t[b] = s
            for h in range(H):
                if h == 2:
                    warm(fill_n[b], s)
                nc.tensor.matmul(s[:, h, :], lhsT=qkT_t[b][:, 0, h, :], rhs=qkT_t[b][:, 1, h, :], start=True, stop=True)

        def st_MAX(b):
            mx = small.tile([P, H], F32, name="mx")
            nc.vector.tensor_reduce(out=mx[:], in_=s_t[b][:], axis=AX.X, op=ALU.max)
            mx_t[b] = mx

        def st_NM(b):
            nm = small.tile([P, H], F32, name="nm")
            nc.scalar.mul(out=nm[:], in_=mx_t[b][:], mul=-SCALE)
            nm_t[b] = nm

        def st_EXP(b):
            u, x = divmod(b, 2)
            e = work.tile([P, H, N], F32, name="e")
            if x == 0:
                z_t[u] = small.tile([P, 2, H], F32, name="z")
            for h in range(H):
                nc.scalar.activation(
                    out=e[:, h, :].rearrange("p (j t) -> p j t", t=T4),
                    in_=s_t[b][:, h, :].rearrange("p (t j) -> p j t", t=T4),
                    func=ACTF.Exp,
                    bias=nm_t[b][:, h:h + 1],
                    scale=SCALE,
                    accum_out=z_t[u][:, x, h:h + 1],
                )
            e_t[b] = e

        def st_REC(u):
            r_t[u] = rf[u % RFN]
            nc.vector.reciprocal(out=r_t[u][:, :, :, 0], in_=z_t[u][:])

        def st_R1(u):
            rb = small.tile([P, 2, H, 2], BF16, name="rb")
            nc.vector.tensor_copy(out=rb[:, :, :, 0], in_=r_t[u][:, :, :, 0])
            rb_t[u] = rb

        def st_R2(u):
            nc.vector.tensor_tensor(out=rb_t[u][:, :, :, 1], in0=r_t[u][:, :, :, 0], in1=rb_t[u][:, :, :, 0], op=ALU.subtract)

        def hi_of(b):
            return e_t[b][:].rearrange("p h m -> p (h m)").bitcast(BF16).rearrange("p (c two) -> p c two", two=2)[:, :, 1]

        def st_LO(b):
            lo = work.tile([P, XS * P], BF16, name="lo")
            nc.vector.tensor_tensor(
                out=lo[:],
                in0=e_t[b][:].rearrange("p h m -> p (h m)")[:, 0:XS * P],
                in1=hi_of(b)[:, 0:XS * P],
                op=ALU.subtract,
            )
            lo_t[b] = lo

        def st_C(b, ts):
            u, x = divmod(b, 2)
            if u not in pc_t:
                pc_t[u] = ps_c.tile([P, 2, T4, NC], F32, name="pc")
            for t in ts:
                if t < XS:
                    nc.tensor.matmul(pc_t[u][:, x, t, 0:2], lhsT=hi_of(b)[:, t * P:(t + 1) * P], rhs=rb_t[u][:, x, t, :], start=True, stop=False)
                    nc.tensor.matmul(pc_t[u][:, x, t, 0:1], lhsT=lo_t[b][:, t * P:(t + 1) * P], rhs=rb_t[u][:, x, t, 0:1], start=False, stop=True)
                else:
                    ncf = NCF[t - XS]
                    nc.tensor.matmul(
                        pc_t[u][:, x, t, 0:ncf].rearrange("p (c a) -> p c a", a=2),
                        lhsT=e_t[b][:, t, :],
                        rhs=r_t[u][:, x, t, :].unsqueeze(1).to_broadcast([P, ncf // 2, 2]),
                        start=True,
                        stop=True,
                    )

        def st_SELb(u):
            c4 = small.tile([P, 2 * T4], F32, name="c4")
            nc.vector.tensor_reduce(out=c4[:], in_=pc_t[u][:, :, :, 0:2].rearrange("p b t c -> p (b t) c"), axis=AX.X, op=ALU.add)
            c4_t[u] = c4

        def st_MUL(b):
            u, x = divmod(b, 2)
            a = apool.tile([P, T4, DH], BF16, name="a")
            for t in range(T4):
                if t < MULP:
                    nc.gpsimd.tensor_scalar(
                        out=a[:, t, :],
                        in0=v_sb[u][:, x * H + t, :],
                        scalar1=c4_t[u][:, x * T4 + t:x * T4 + t + 1],
                        scalar2=0.0,
                        op0=ALU.mult,
                        op1=ALU.add,
                    )
                else:
                    nc.vector.tensor_scalar(
                        out=a[:, t, :],
                        in0=v_sb[u][:, x * H + t, :],
                        scalar1=c4_t[u][:, x * T4 + t:x * T4 + t + 1],
                        scalar2=None,
                        op0=ALU.mult,
                    )
            a_t[b] = a

        def st_AT(b):
            u, x = divmod(b, 2)
            xt_t[b] = xt_all[:, x, :, :]
            words = a_t[b][:].rearrange("p h d -> p (h d)").bitcast(F32)
            for w2 in range(2):
                nc.tensor.transpose(xt_t[b][:, w2, :], words[:, w2 * P:(w2 + 1) * P], ident32[:])

        def st_XEV(b):
            u, x = divmod(b, 2)
            grp = mxp.tile([P, N * H], BF16, name="grp", align_bytes=64)
            nc.scalar.copy(
                out=grp[:].bitcast(F32).rearrange("p (m w) -> p m w", w=2),
                in_=xt_t[b].rearrange("p w m -> p m w"),
            )
            grp_t[b] = grp

        def st_QZ(b):
            cod = mxp.tile([P, N], U32, name="cod", align_bytes=64)
            scl = mxp.tile([P, N], U8, name="scl", align_bytes=64)
            nc.vector.quantize_mx(out=cod[:].bitcast(FP8X4), scales=scl[:], in_=grp_t[b][:])
            cod_t[b] = cod
            scl_t[b] = scl

        def st_MX(b):
            u, x = divmod(b, 2)
            po_t[b] = po_all[:, x, :]
            nc.tensor.matmul_mx(
                out=po_t[b],
                lhsT=cod_t[b][:].bitcast(FP8X4),
                lhsT_scale=scl_t[b][:],
                rhs=w_cod[:].bitcast(FP8X4),
                rhs_scale=w_scl[:],
                start=True,
                stop=True,
            )

        def st_OUT(b):
            u, x = divmod(b, 2)
            o = outp.tile([P, D], F32, name="o")
            nc.vector.tensor_tensor(out=o[:], in0=po_t[b], in1=bias[:], op=ALU.add)
            nc.sync.dma_start(out=out[b], in_=o[:])

        def st_C0(b):
            st_C(b, (0, 1))

        def st_C1(b):
            st_C(b, (2, 3))

        order = (
            (
                (st_OUT, 13, False),
                (st_R2, 5, True),
                (st_SELb, 7, True),
                (st_MAX, 2, False),
                (st_LO, 4, False),
                (st_QZ, 11, False),
                (st_MUL, 8, False),
                (st_EXP, 3, False),
                (st_XEV, 10, False),
                (st_NM, 2, False),
                (st_T, 0, False),
                (st_EV, 0, False),
                (st_QK, 1, False),
                (st_C0, 6, False),
                (st_MX, 12, False),
                (st_C1, 6, False),
                (st_AT, 9, False),
            ),
            (
                (st_OUT, 13, False),
                (st_MAX, 2, False),
                (st_REC, 4, True),
                (st_LO, 4, False),
                (st_R1, 4, True),
                (st_QZ, 11, False),
                (st_MUL, 8, False),
                (st_EXP, 3, False),
                (st_XEV, 10, False),
                (st_NM, 2, False),
                (st_T, 0, False),
                (st_EV, 0, False),
                (st_QK, 1, False),
                (st_C0, 6, False),
                (st_MX, 12, False),
                (st_C1, 6, False),
                (st_AT, 9, False),
            ),
        )
        last = max(lag for half in order for st, lag, pair in half)
        for k in range(B + last + 1):
            if k % 2 == 0 and k // 2 + PRE < NP:
                load(k // 2 + PRE)
            if k == 8:
                prep_w()
            counted = 0
            for st, lag, pair in order[k % 2]:
                if 0 <= k - lag < B:
                    if st == st_QK:
                        counted += H * N
                    if st == st_MX:
                        counted += D
                    if st == st_C0:
                        counted += XS * 3 + 4 * sum(NCF)
            for st, lag, pair in order[k % 2]:
                if st == st_QK:
                    fill_n[k - lag] = max(0, TARGET - counted)
            for st, lag, pair in order[k % 2]:
                i = k - lag
                if pair:
                    assert i % 2 == 1
                    if 0 <= i // 2 < NP:
                        st(i // 2)
                elif 0 <= i < B:
                    st(i)
